import numpy as np
import ml_dtypes


def mxq(x, axis, fmt="e4m3"):
    dtype, down = {"e4m3": (ml_dtypes.float8_e4m3fn, 7), "e5m2": (ml_dtypes.float8_e5m2, 14)}[fmt]
    v = np.moveaxis(np.asarray(x, np.float32).astype(ml_dtypes.bfloat16).astype(np.float64), axis, -1)
    blocks = v.reshape(v.shape[:-1] + (-1, 32))
    amax = np.abs(blocks).max(-1, keepdims=True)
    byte = np.maximum(np.where(amax > 0, np.frexp(amax)[1] - 1 + 127, 0) - down, 1)
    scale = np.exp2(byte - 127.0)
    codes = (blocks / scale).astype(np.float32).astype(dtype).astype(np.float64)
    return np.moveaxis((codes * scale).reshape(v.shape), -1, axis)


WIDE = False


def mx_kscale(k):
    if not WIDE:
        return np.ones(k)
    levels = np.array([10, -10, 5, -5, 0])
    a = np.random.permutation(np.resize(levels, k // 512 * 4)).reshape(k // 512, 4)
    idx = np.arange(k)
    return np.exp2(a[idx // 512, idx % 128 // 32])


BF16 = ml_dtypes.bfloat16


def bf(x):
    return np.asarray(x, np.float32).astype(BF16)


def f64(x):
    return np.asarray(x).astype(np.float64)


E2M1 = np.array([0.0, 0.5, 1.0, 1.5, 2.0, 3.0, 4.0, 6.0, -0.0, -0.5, -1.0, -1.5, -2.0, -3.0, -4.0, -6.0])


def pack_weight(w, fmt):
    k, n = w.shape
    w = f64(bf(w)).reshape(k // 32, 32, n)
    amax = np.abs(w).max(1)
    if fmt == "e4m3":
        byte = np.frexp(amax)[1] - 1 + 127 - 7
    else:
        mant, ex = np.frexp(amax / 6.0)
        byte = np.where(mant > 0.5, ex, ex - 1) + 127
    byte = np.clip(np.where(amax > 0, byte, 1), 1, 254)
    scaled = (w * np.exp2(127.0 - byte)[:, None, :]).reshape(k, n).astype(np.float32)
    by_word = np.ascontiguousarray(scaled.reshape(k // 512, 128, 4, n).transpose(0, 1, 3, 2))
    if fmt == "e4m3":
        words = by_word.astype(ml_dtypes.float8_e4m3fn).view(np.uint8)
    else:
        c = by_word.astype(ml_dtypes.float4_e2m1fn).view(np.uint8) & 0xF
        words = c[..., 0::2] | (c[..., 1::2] << 4)
    return np.ascontiguousarray(words), np.ascontiguousarray(byte.astype(np.uint8).reshape(k // 512, 16, n))


def unpack_weight(words, scales, fmt):
    g, p, n, _ = words.shape
    if fmt == "e4m3":
        vals = np.ascontiguousarray(words).view(ml_dtypes.float8_e4m3fn).astype(np.float64)
    else:
        nib = np.empty((g, p, n, 4), np.uint8)
        nib[..., 0::2] = words & 0xF
        nib[..., 1::2] = words >> 4
        vals = E2M1[nib]
    vals = vals * np.repeat(np.exp2(scales.astype(np.float64) - 127.0), 8, axis=1)[..., None]
    return vals.transpose(0, 1, 3, 2).reshape(g * 512, n)


B, C, H, W, S, HID, OC = 2, 512, 16, 16, 2, 4096, 2048
H2, W2 = H // S, W // S
K1 = C * S * S
RESIDUAL = True
FMT = "e4m3"


def setup_inputs():
    s = mx_kscale(K1)
    s = s / s.max()
    sx = np.broadcast_to(s.reshape(C, 1, S, 1, S), (C, H2, S, W2, S)).reshape(C, H, W)
    x = bf(np.random.standard_normal((B, C, H, W)) * sx)
    w1 = np.random.standard_normal((HID, K1)) / np.sqrt(K1) / s
    weight1_words, weight1_scales = pack_weight(np.ascontiguousarray(w1.T), FMT)
    bias1 = bf(np.random.standard_normal(HID) * 0.2)
    w2 = np.random.standard_normal((OC, HID)) * 1.5 / np.sqrt(HID)
    weight2_words, weight2_scales = pack_weight(np.ascontiguousarray(w2.T), FMT)
    bias2 = bf(np.random.standard_normal(OC) * 0.2)
    return {"x": x,
            "weight1_words": weight1_words,
            "weight1_scales": weight1_scales,
            "bias1": bias1,
            "weight2_words": weight2_words,
            "weight2_scales": weight2_scales,
            "bias2": bias2}


def reference(x, weight1_words, weight1_scales, bias1, weight2_words, weight2_scales, bias2):
    x = f64(x)
    p = x.reshape(B, C, H2, S, W2, S)
    p = p.transpose(0, 2, 4, 1, 3, 5).reshape(B * H2 * W2, C * S * S)
    o1 = (mxq(p, 1, "e4m3") @ unpack_weight(weight1_words, weight1_scales, FMT)) + f64(bias1)
    o2 = o1 * (1.0 / (1.0 + np.exp(-o1)))
    o3 = (mxq(o2, 1, "e4m3") @ unpack_weight(weight2_words, weight2_scales, FMT)) + f64(bias2)
    out = o3.reshape(B, H2, W2, -1).transpose(0, 3, 1, 2)
    if RESIDUAL:
        pooled = x.reshape(B, C, H2, S, W2, S).mean(axis=(3, 5))
        n = out.shape[1] // C
        res = np.repeat(pooled, n, axis=1)
        out = out + res
    return out

@@ -1,0 +1,201 @@
+from contextlib import ExitStack
+
+import concourse.mybir as mybir
+from concourse.masks import make_identity
+
+F32 = mybir.dt.float32
+BF16 = mybir.dt.bfloat16
+I32 = mybir.dt.int32
+U32 = mybir.dt.uint32
+U8 = mybir.dt.uint8
+FP8X4 = mybir.dt.float8_e4m3fn_x4
+ACT = mybir.ActivationFunctionType
+ALU = mybir.AluOpType
+
+P = 128
+HID = 4096
+OC = 2048
+K1 = 2048
+FLOPS = 2 * P * K1 * HID + 2 * P * HID * OC
+
+W1_CHUNKS = ((0, 2048), (2048, 1024), (3072, 1024))
+
+
+def tile_memoryefficientpatchdownscale_w_kernel(
+    tc, x, weight1_words, weight1_scales, bias1, weight2_words, weight2_scales, bias2, out
+):
+    nc = tc.nc
+    with ExitStack() as ctx:
+        keep = ctx.enter_context(tc.tile_pool(name="keep", bufs=1))
+        work = ctx.enter_context(tc.tile_pool(name="work", bufs=3))
+        psum = ctx.enter_context(tc.psum_pool(name="psum", bufs=8))
+
+        s1 = keep.tile([P, HID], U8, name="s1", align_bytes=64)
+        s2 = keep.tile([P, 2, OC], U8, name="s2", align_bytes=64)
+        nc.vector.memset(s1[:].bitcast(I32), 0)
+        nc.vector.memset(s2[:].bitcast(I32), 0)
+
+        x_sb = keep.tile([P, 64, 2, 8, 2], BF16, name="x_sb", align_bytes=64)
+        x_dst = x_sb[:].rearrange("p (g b i) u j v -> p g b (i u j v)", g=4, b=2)
+        for b in range(2):
+            nc.sync.dma_start(out=x_dst[:, :, b, :], in_=x[b].rearrange("(g p) h w -> p g (h w)", p=P))
+        for q in range(4):
+            nc.sync.dma_start(
+                out=s1[32 * q : 32 * q + 16, :].bitcast(I32),
+                in_=weight1_scales[:, 4 * q : 4 * q + 4, :].bitcast(I32),
+            )
+        for h in range(2):
+            for q in range(4):
+                nc.sync.dma_start(
+                    out=s2[32 * q : 32 * q + 16, h, :].bitcast(I32),
+                    in_=weight2_scales[4 * h : 4 * h + 4, 4 * q : 4 * q + 4, :].bitcast(I32),
+                )
+        w1t = {}
+        for c, (col0, width) in enumerate(W1_CHUNKS):
+            for kg in range(4):
+                t = keep.tile([P, width], U32, name="w1_%d_%d" % (c, kg), align_bytes=64)
+                src = weight1_words[kg].rearrange("p n t -> p (n t)")[:, 4 * col0 : 4 * (col0 + width)]
+                nc.sync.dma_start(out=t[:].bitcast(I32), in_=src.bitcast(I32))
+                w1t[(c, kg)] = t
+        w2t = {}
+        for hh in range(2):
+            for g2 in range(8):
+                t = keep.tile([P, 1024], U32, name="w2_%d_%d" % (hh, g2), align_bytes=64)
+                src = weight2_words[g2].rearrange("p n t -> p (n t)")[:, 4096 * hh : 4096 * (hh + 1)]
+                nc.sync.dma_start(out=t[:].bitcast(I32), in_=src.bitcast(I32))
+                w2t[(hh, g2)] = t
+
+        b1rows = keep.tile([P, 512], BF16, name="b1rows")
+        nc.vector.memset(b1rows[:], 0.0)
+        nc.scalar.dma_start(out=b1rows[0:8, :], in_=bias1.rearrange("(g f) -> g f", f=512))
+        b2rows = keep.tile([P, P], BF16, name="b2rows")
+        nc.vector.memset(b2rows[:], 0.0)
+        nc.scalar.dma_start(out=b2rows[0:16, :], in_=bias2.rearrange("(j o) -> j o", o=P))
+
+        warm = keep.tile([P, 1], F32, name="warm")
+        nc.vector.memset(warm[:], 0.0)
+        warm2 = keep.tile([P, 1], F32, name="warm2")
+        nc.scalar.activation(out=warm2[:], in_=warm[:], func=ACT.Silu)
+
+        ident = keep.tile([P, P], BF16, name="ident")
+        make_identity(nc, ident[:])
+
+        grouped = keep.tile([P, 64, 8, 2, 2], BF16, name="grouped", align_bytes=64)
+        nc.vector.tensor_copy(
+            out=grouped[:].bitcast(F32)[:, :, :, :, 0],
+            in_=x_sb[:].bitcast(F32)[:, :, :, :, 0].rearrange("p s u j -> p s j u"),
+        )
+        p_codes = keep.tile([P, 512], U32, name="p_codes", align_bytes=64)
+        p_plane = keep.tile([P, 512], U8, name="p_plane", align_bytes=64)
+        nc.vector.quantize_mx(
+            out=p_codes[:].bitcast(FP8X4),
+            scales=p_plane[:],
+            in_=grouped[:].rearrange("p s j u v -> p (s j u v)"),
+        )
+
+        b1bc = keep.tile([P, 8, 4, P], BF16, name="b1bc")
+        for g in range(8):
+            ps = psum.tile([P, 512], F32, name="ps_b1", tag="bank")
+            nc.tensor.matmul(
+                out=ps[:], lhsT=ident[:, g : g + 1].to_broadcast([P, P]), rhs=b1rows[:], start=True, stop=True
+            )
+            nc.scalar.copy(out=b1bc[:, g], in_=ps[:].rearrange("m (p t) -> m t p", t=4))
+
+        ps_b2 = psum.tile([P, 512], F32, name="ps_b2", tag="bank")
+        nc.tensor.transpose(ps_b2[:].bitcast(BF16)[:, 0:P], b2rows[:], ident[:])
+        b2col = keep.tile([P, 16], F32, name="b2col")
+        nc.vector.tensor_copy(out=b2col[:], in_=ps_b2[:].bitcast(BF16)[:, 0:16])
+
+        rsel = keep.tile([P, P, 4], BF16, name="rsel")
+        nc.vector.tensor_scalar_mul(out=rsel[:], in0=ident[:].unsqueeze(2).to_broadcast([P, P, 4]), scalar1=0.25)
+        rflat = rsel[:].rearrange("c q r -> c (q r)")
+        resb = keep.tile([P, 16, P], F32, name="resb")
+        for a in range(4):
+            ps = psum.tile([P, 512], F32, name="ps_res", tag="bank")
+            for n in range(4):
+                nc.tensor.matmul(
+                    out=ps[:].rearrange("o (s j) -> o s j", j=8),
+                    lhsT=rflat[:, P * a : P * a + P],
+                    rhs=x_sb[:, :, n // 2, :, n % 2],
+                    start=(n == 0),
+                    stop=(n == 3),
+                )
+            nc.vector.tensor_tensor(
+                out=resb[:, a:16:4, :],
+                in0=ps[:].rearrange("o (g r) -> o g r", g=4),
+                in1=b2col[:, a:16:4].unsqueeze(2).to_broadcast([P, 4, P]),
+                op=ALU.add,
+            )
+
+        og = keep.tile([P, 8, P, 4], BF16, name="og", align_bytes=64)
+        o2_codes = keep.tile([P, 8, P], U32, name="o2_codes", align_bytes=64)
+        o2_plane = keep.tile([P, 8, P], U8, name="o2_plane", align_bytes=64)
+        for c, (col0, width) in enumerate(W1_CHUNKS):
+            nb = width // 512
+            banks = []
+            for n in range(nb):
+                bank = psum.tile([P, 512], F32, name="ps_o1", tag="bank")
+                banks.append(bank)
+            for kg in range(4):
+                for n in range(nb):
+                    nc.tensor.matmul_mx(
+                        out=banks[n][:],
+                        lhsT=p_codes[:, P * kg : P * kg + P].bitcast(FP8X4),
+                        lhsT_scale=p_plane[:, P * kg : P * kg + P],
+                        rhs=w1t[(c, kg)][:, 512 * n : 512 * n + 512].bitcast(FP8X4),
+                        rhs_scale=s1[4 * kg : P, col0 + 512 * n : col0 + 512 * n + 512],
+                        start=(kg == 0),
+                        stop=(kg == 3),
+                    )
+            for n in range(nb):
+                g2 = col0 // 512 + n
+                o1 = work.tile([P, 4, P], F32, name="o1")
+                nc.vector.tensor_tensor(
+                    out=o1[:], in0=banks[n][:].rearrange("m (p t) -> m t p", t=4), in1=b1bc[:, g2], op=ALU.add
+                )
+                o2 = work.tile([P, 4, P], BF16, name="o2")
+                nc.scalar.activation(out=o2[:], in_=o1[:], func=ACT.Silu)
+                pt = psum.tile([P, 512], F32, name="ps_t", tag="bank")
+                ptb = pt[:].bitcast(BF16)
+                for t in range(4):
+                    nc.tensor.transpose(ptb[:, P * t : P * t + P], o2[:, t, :], ident[:])
+                src = ptb[:, 0:512].rearrange("p (t r) -> p r t", t=4)
+                if g2 % 3 == 2:
+                    nc.vector.tensor_copy(out=og[:, g2], in_=src)
+                else:
+                    nc.scalar.copy(out=og[:, g2], in_=src)
+                nc.vector.quantize_mx(
+                    out=o2_codes[:, g2, :].bitcast(FP8X4),
+                    scales=o2_plane[:, g2, :],
+                    in_=og[:, g2].rearrange("p r t -> p (r t)"),
+                )
+
+        out_sb = keep.tile([P, 2, 2, 8, 64], F32, name="out_sb")
+        for hh in range(2):
+            accs = []
+            for j in range(8):
+                acc = psum.tile([P, 512], F32, name="ps_o3", tag="bank")
+                accs.append(acc)
+            for g2 in range(8):
+                for j in range(8):
+                    nc.tensor.matmul_mx(
+                        out=accs[j][:, 0:P],
+                        lhsT=w2t[(hh, g2)][:, P * j : P * j + P].bitcast(FP8X4),
+                        lhsT_scale=s2[4 * (g2 % 4) : P, g2 // 4, 1024 * hh + P * j : 1024 * hh + P * j + P],
+                        rhs=o2_codes[:, g2, :].bitcast(FP8X4),
+                        rhs_scale=o2_plane[:, g2, :],
+                        start=(g2 == 0),
+                        stop=(g2 == 7),
+                    )
+            for j in range(8):
+                nc.vector.tensor_tensor(
+                    out=out_sb[:, hh, :, j, :],
+                    in0=accs[j][:, 0:P].rearrange("o (b s) -> o b s", b=2),
+                    in1=resb[:, 8 * hh + j, :].rearrange("o (b s) -> o b s", b=2),
+                    op=ALU.add,
+                )
+            for b in range(2):
+                nc.sync.dma_start(
+                    out=out[b, 1024 * hh : 1024 * hh + 1024].rearrange("(j o) h w -> o j (h w)", o=P),
+                    in_=out_sb[:, hh, b],
+                )

@@ -35,21 +35,24 @@ def tile_memoryefficientpatchdownscale_w_kernel(
         nc.vector.memset(s1[:].bitcast(I32), 0)
         nc.vector.memset(s2[:].bitcast(I32), 0)
 
+        ident = keep.tile([P, P], BF16, name="ident")
+        make_identity(nc, ident[:])
+
+        for q in range(4):
+            nc.gpsimd.dma_start(
+                out=s1[32 * q : 32 * q + 16, :].bitcast(F32),
+                in_=weight1_scales[:, 4 * q : 4 * q + 4, :].bitcast(F32),
+            )
+        for h in range(2):
+            for q in range(4):
+                nc.gpsimd.dma_start(
+                    out=s2[32 * q : 32 * q + 16, h, :].bitcast(F32),
+                    in_=weight2_scales[4 * h : 4 * h + 4, 4 * q : 4 * q + 4, :].bitcast(F32),
+                )
         x_sb = keep.tile([P, 64, 2, 8, 2], BF16, name="x_sb", align_bytes=64)
         x_dst = x_sb[:].rearrange("p (g b i) u j v -> p g b (i u j v)", g=4, b=2)
         for b in range(2):
             nc.sync.dma_start(out=x_dst[:, :, b, :], in_=x[b].rearrange("(g p) h w -> p g (h w)", p=P))
-        for q in range(4):
-            nc.sync.dma_start(
-                out=s1[32 * q : 32 * q + 16, :].bitcast(I32),
-                in_=weight1_scales[:, 4 * q : 4 * q + 4, :].bitcast(I32),
-            )
-        for h in range(2):
-            for q in range(4):
-                nc.sync.dma_start(
-                    out=s2[32 * q : 32 * q + 16, h, :].bitcast(I32),
-                    in_=weight2_scales[4 * h : 4 * h + 4, 4 * q : 4 * q + 4, :].bitcast(I32),
-                )
         w1t = {}
         for c, (col0, width) in enumerate(W1_CHUNKS):
             for kg in range(4):
@@ -76,9 +79,6 @@ def tile_memoryefficientpatchdownscale_w_kernel(
         nc.vector.memset(warm[:], 0.0)
         warm2 = keep.tile([P, 1], F32, name="warm2")
         nc.scalar.activation(out=warm2[:], in_=warm[:], func=ACT.Silu)
-
-        ident = keep.tile([P, P], BF16, name="ident")
-        make_identity(nc, ident[:])
 
         grouped = keep.tile([P, 64, 8, 2, 2], BF16, name="grouped", align_bytes=64)
         nc.vector.tensor_copy(

@@ -19,6 +19,7 @@ K1 = 2048
 FLOPS = 2 * P * K1 * HID + 2 * P * HID * OC
 
 W1_CHUNKS = ((0, 2048), (2048, 1024), (3072, 1024))
+W2_GROUPS = ((0, 6), (6, 8), (14, 2))
 
 
 def tile_memoryefficientpatchdownscale_w_kernel(
@@ -27,17 +28,26 @@ def tile_memoryefficientpatchdownscale_w_kernel(
     nc = tc.nc
     with ExitStack() as ctx:
         keep = ctx.enter_context(tc.tile_pool(name="keep", bufs=1))
-        work = ctx.enter_context(tc.tile_pool(name="work", bufs=3))
+        work = ctx.enter_context(tc.tile_pool(name="work", bufs=4))
         psum = ctx.enter_context(tc.psum_pool(name="psum", bufs=8))
+        ctx.enter_context(tc.manual_schedule())
 
+        b1rows = keep.tile([P, 512], BF16, name="b1rows")
+        b2rows = keep.tile([P, P], BF16, name="b2rows")
         s1 = keep.tile([P, HID], U8, name="s1", align_bytes=64)
         s2 = keep.tile([P, 2, OC], U8, name="s2", align_bytes=64)
+        warm = keep.tile([P, 1], F32, name="warm")
+        nc.vector.memset(b1rows[:], 0.0)
+        nc.vector.memset(b2rows[:], 0.0)
         nc.vector.memset(s1[:].bitcast(I32), 0)
         nc.vector.memset(s2[:].bitcast(I32), 0)
+        nc.vector.memset(warm[:], 0.0)
+
+        warm2 = keep.tile([P, 1], F32, name="warm2")
+        nc.scalar.activation(out=warm2[:], in_=warm[:], func=ACT.Silu)
 
         ident = keep.tile([P, P], BF16, name="ident")
         make_identity(nc, ident[:])
-
         for q in range(4):
             nc.gpsimd.dma_start(
                 out=s1[32 * q : 32 * q + 16, :].bitcast(F32),
@@ -49,10 +59,13 @@ def tile_memoryefficientpatchdownscale_w_kernel(
                     out=s2[32 * q : 32 * q + 16, h, :].bitcast(F32),
                     in_=weight2_scales[4 * h : 4 * h + 4, 4 * q : 4 * q + 4, :].bitcast(F32),
                 )
+
         x_sb = keep.tile([P, 64, 2, 8, 2], BF16, name="x_sb", align_bytes=64)
         x_dst = x_sb[:].rearrange("p (g b i) u j v -> p g b (i u j v)", g=4, b=2)
         for b in range(2):
             nc.sync.dma_start(out=x_dst[:, :, b, :], in_=x[b].rearrange("(g p) h w -> p g (h w)", p=P))
+        nc.sync.dma_start(out=b2rows[0:16, :], in_=bias2.rearrange("(j o) -> j o", o=P))
+        nc.sync.dma_start(out=b1rows[0:8, :], in_=bias1.rearrange("(g f) -> g f", f=512))
         w1t = {}
         for c, (col0, width) in enumerate(W1_CHUNKS):
             for kg in range(4):
@@ -61,25 +74,24 @@ def tile_memoryefficientpatchdownscale_w_kernel(
                 nc.sync.dma_start(out=t[:].bitcast(I32), in_=src.bitcast(I32))
                 w1t[(c, kg)] = t
         w2t = {}
-        for hh in range(2):
+        for grp in range(2):
+            j0, cnt = W2_GROUPS[grp]
             for g2 in range(8):
-                t = keep.tile([P, 1024], U32, name="w2_%d_%d" % (hh, g2), align_bytes=64)
-                src = weight2_words[g2].rearrange("p n t -> p (n t)")[:, 4096 * hh : 4096 * (hh + 1)]
+                t = keep.tile([P, P * cnt], U32, name="w2_%d_%d" % (grp, g2), align_bytes=64)
+                src = weight2_words[g2].rearrange("p n t -> p (n t)")[:, 4 * P * j0 : 4 * P * (j0 + cnt)]
                 nc.sync.dma_start(out=t[:].bitcast(I32), in_=src.bitcast(I32))
-                w2t[(hh, g2)] = t
+                w2t[(grp, g2)] = t[:]
+        j0, cnt = W2_GROUPS[2]
+        for h in range(2):
+            t = keep.tile([P, 4, P * cnt], U32, name="w2_2_%d" % h, align_bytes=64)
+            src = weight2_words[4 * h : 4 * h + 4].rearrange("g p n t -> p g (n t)")
+            nc.sync.dma_start(out=t[:].bitcast(I32), in_=src[:, :, 4 * P * j0 : 4 * P * (j0 + cnt)].bitcast(I32))
+            for gl in range(4):
+                w2t[(2, 4 * h + gl)] = t[:, gl, :]
 
-        b1rows = keep.tile([P, 512], BF16, name="b1rows")
-        nc.vector.memset(b1rows[:], 0.0)
-        nc.scalar.dma_start(out=b1rows[0:8, :], in_=bias1.rearrange("(g f) -> g f", f=512))
-        b2rows = keep.tile([P, P], BF16, name="b2rows")
-        nc.vector.memset(b2rows[:], 0.0)
-        nc.scalar.dma_start(out=b2rows[0:16, :], in_=bias2.rearrange("(j o) -> j o", o=P))
-
-        warm = keep.tile([P, 1], F32, name="warm")
-        nc.vector.memset(warm[:], 0.0)
-        warm2 = keep.tile([P, 1], F32, name="warm2")
-        nc.scalar.activation(out=warm2[:], in_=warm[:], func=ACT.Silu)
-
+        rsel = keep.tile([P, P, 4], BF16, name="rsel")
+        nc.vector.tensor_scalar_mul(out=rsel[:], in0=ident[:].unsqueeze(2).to_broadcast([P, P, 4]), scalar1=0.25)
+        rflat = rsel[:].rearrange("c q r -> c (q r)")
         grouped = keep.tile([P, 64, 8, 2, 2], BF16, name="grouped", align_bytes=64)
         nc.vector.tensor_copy(
             out=grouped[:].bitcast(F32)[:, :, :, :, 0],
@@ -93,23 +105,8 @@ def tile_memoryefficientpatchdownscale_w_kernel(
             in_=grouped[:].rearrange("p s j u v -> p (s j u v)"),
         )
 
-        b1bc = keep.tile([P, 8, 4, P], BF16, name="b1bc")
-        for g in range(8):
-            ps = psum.tile([P, 512], F32, name="ps_b1", tag="bank")
-            nc.tensor.matmul(
-                out=ps[:], lhsT=ident[:, g : g + 1].to_broadcast([P, P]), rhs=b1rows[:], start=True, stop=True
-            )
-            nc.scalar.copy(out=b1bc[:, g], in_=ps[:].rearrange("m (p t) -> m t p", t=4))
-
-        ps_b2 = psum.tile([P, 512], F32, name="ps_b2", tag="bank")
-        nc.tensor.transpose(ps_b2[:].bitcast(BF16)[:, 0:P], b2rows[:], ident[:])
-        b2col = keep.tile([P, 16], F32, name="b2col")
-        nc.vector.tensor_copy(out=b2col[:], in_=ps_b2[:].bitcast(BF16)[:, 0:16])
-
-        rsel = keep.tile([P, P, 4], BF16, name="rsel")
-        nc.vector.tensor_scalar_mul(out=rsel[:], in0=ident[:].unsqueeze(2).to_broadcast([P, P, 4]), scalar1=0.25)
-        rflat = rsel[:].rearrange("c q r -> c (q r)")
         resb = keep.tile([P, 16, P], F32, name="resb")
+        res_ps = []
         for a in range(4):
             ps = psum.tile([P, 512], F32, name="ps_res", tag="bank")
             for n in range(4):
@@ -120,82 +117,156 @@ def tile_memoryefficientpatchdownscale_w_kernel(
                     start=(n == 0),
                     stop=(n == 3),
                 )
+            res_ps.append(ps)
+
+        ps_b2 = psum.tile([P, 512], F32, name="ps_b2", tag="bank")
+        nc.tensor.transpose(ps_b2[:].bitcast(BF16)[:, 0:P], b2rows[:], ident[:])
+        b2col = keep.tile([P, 16], F32, name="b2col")
+        nc.vector.tensor_copy(out=b2col[:], in_=ps_b2[:].bitcast(BF16)[:, 0:16])
+
+        for a in range(4):
             nc.vector.tensor_tensor(
                 out=resb[:, a:16:4, :],
-                in0=ps[:].rearrange("o (g r) -> o g r", g=4),
+                in0=res_ps[a][:].rearrange("o (g r) -> o g r", g=4),
                 in1=b2col[:, a:16:4].unsqueeze(2).to_broadcast([P, 4, P]),
                 op=ALU.add,
             )
 
+        b1bc = keep.tile([P, 8, 4, P], BF16, name="b1bc")
+        for g in range(8):
+            ps = psum.tile([P, 512], F32, name="ps_b1", tag="bank")
+            nc.tensor.matmul(
+                out=ps[:], lhsT=ident[:, g : g + 1].to_broadcast([P, P]), rhs=b1rows[:], start=True, stop=True
+            )
+            nc.scalar.copy(out=b1bc[:, g], in_=ps[:].rearrange("m (p t) -> m t p", t=4))
+
         og = keep.tile([P, 8, P, 4], BF16, name="og", align_bytes=64)
         o2_codes = keep.tile([P, 8, P], U32, name="o2_codes", align_bytes=64)
         o2_plane = keep.tile([P, 8, P], U8, name="o2_plane", align_bytes=64)
-        for c, (col0, width) in enumerate(W1_CHUNKS):
-            nb = width // 512
-            banks = []
-            for n in range(nb):
-                bank = psum.tile([P, 512], F32, name="ps_o1", tag="bank")
-                banks.append(bank)
-            for kg in range(4):
-                for n in range(nb):
-                    nc.tensor.matmul_mx(
-                        out=banks[n][:],
-                        lhsT=p_codes[:, P * kg : P * kg + P].bitcast(FP8X4),
-                        lhsT_scale=p_plane[:, P * kg : P * kg + P],
-                        rhs=w1t[(c, kg)][:, 512 * n : 512 * n + 512].bitcast(FP8X4),
-                        rhs_scale=s1[4 * kg : P, col0 + 512 * n : col0 + 512 * n + 512],
-                        start=(kg == 0),
-                        stop=(kg == 3),
-                    )
-            for n in range(nb):
+        out_sb = keep.tile([P, 2, 16, 64], F32, name="out_sb")
+        banks = {}
+        o2s = {}
+        pts = {}
+        accs = {}
+
+        def mm1(c, kg):
+            col0, width = W1_CHUNKS[c]
+            for n in range(width // 512):
                 g2 = col0 // 512 + n
-                o1 = work.tile([P, 4, P], F32, name="o1")
-                nc.vector.tensor_tensor(
-                    out=o1[:], in0=banks[n][:].rearrange("m (p t) -> m t p", t=4), in1=b1bc[:, g2], op=ALU.add
-                )
-                o2 = work.tile([P, 4, P], BF16, name="o2")
-                nc.scalar.activation(out=o2[:], in_=o1[:], func=ACT.Silu)
-                pt = psum.tile([P, 512], F32, name="ps_t", tag="bank")
-                ptb = pt[:].bitcast(BF16)
-                for t in range(4):
-                    nc.tensor.transpose(ptb[:, P * t : P * t + P], o2[:, t, :], ident[:])
-                src = ptb[:, 0:512].rearrange("p (t r) -> p r t", t=4)
-                if g2 % 3 == 2:
-                    nc.vector.tensor_copy(out=og[:, g2], in_=src)
-                else:
-                    nc.scalar.copy(out=og[:, g2], in_=src)
-                nc.vector.quantize_mx(
-                    out=o2_codes[:, g2, :].bitcast(FP8X4),
-                    scales=o2_plane[:, g2, :],
-                    in_=og[:, g2].rearrange("p r t -> p (r t)"),
+                if kg == 0:
+                    bank = psum.tile([P, 512], F32, name="ps_o1", tag="bank")
+                    banks[g2] = bank
+                nc.tensor.matmul_mx(
+                    out=banks[g2][:],
+                    lhsT=p_codes[:, P * kg : P * kg + P].bitcast(FP8X4),
+                    lhsT_scale=p_plane[:, P * kg : P * kg + P],
+                    rhs=w1t[(c, kg)][:, 512 * n : 512 * n + 512].bitcast(FP8X4),
+                    rhs_scale=s1[4 * kg : P, 512 * g2 : 512 * g2 + 512],
+                    start=(kg == 0),
+                    stop=(kg == 3),
                 )
 
-        out_sb = keep.tile([P, 2, 2, 8, 64], F32, name="out_sb")
-        for hh in range(2):
-            accs = []
-            for j in range(8):
-                acc = psum.tile([P, 512], F32, name="ps_o3", tag="bank")
-                accs.append(acc)
-            for g2 in range(8):
-                for j in range(8):
-                    nc.tensor.matmul_mx(
-                        out=accs[j][:, 0:P],
-                        lhsT=w2t[(hh, g2)][:, P * j : P * j + P].bitcast(FP8X4),
-                        lhsT_scale=s2[4 * (g2 % 4) : P, g2 // 4, 1024 * hh + P * j : 1024 * hh + P * j + P],
-                        rhs=o2_codes[:, g2, :].bitcast(FP8X4),
-                        rhs_scale=o2_plane[:, g2, :],
-                        start=(g2 == 0),
-                        stop=(g2 == 7),
-                    )
-            for j in range(8):
+        def act(g2):
+            o1 = work.tile([P, 4, P], F32, name="o1")
+            nc.vector.tensor_tensor(
+                out=o1[:], in0=banks[g2][:].rearrange("m (p t) -> m t p", t=4), in1=b1bc[:, g2], op=ALU.add
+            )
+            o2 = work.tile([P, 4, P], BF16, name="o2")
+            nc.scalar.activation(out=o2[:], in_=o1[:], func=ACT.Silu)
+            o2s[g2] = o2
+
+        def tr(g2):
+            pt = psum.tile([P, 512], F32, name="ps_t", tag="bank")
+            for t in range(4):
+                nc.tensor.transpose(pt[:].bitcast(BF16)[:, P * t : P * t + P], o2s[g2][:, t, :], ident[:])
+            pts[g2] = pt
+
+        def cq(g2):
+            src = pts[g2][:].bitcast(BF16)[:, 0:512].rearrange("p (t r) -> p r t", t=4)
+            if g2 % 3 == 2:
+                nc.vector.tensor_copy(out=og[:, g2], in_=src)
+            else:
+                nc.scalar.copy(out=og[:, g2], in_=src)
+            nc.vector.quantize_mx(
+                out=o2_codes[:, g2, :].bitcast(FP8X4),
+                scales=o2_plane[:, g2, :],
+                in_=og[:, g2].rearrange("p r t -> p (r t)"),
+            )
+
+        def mm2(grp, g2):
+            j0, cnt = W2_GROUPS[grp]
+            for jj in range(cnt):
+                j = j0 + jj
+                if g2 == 0:
+                    acc = psum.tile([P, 512], F32, name="ps_o3", tag="bank")
+                    accs[j] = acc
+                nc.tensor.matmul_mx(
+                    out=accs[j][:, 0:P],
+                    lhsT=w2t[(grp, g2)][:, P * jj : P * jj + P].bitcast(FP8X4),
+                    lhsT_scale=s2[4 * (g2 % 4) : P, g2 // 4, P * j : P * j + P],
+                    rhs=o2_codes[:, g2, :].bitcast(FP8X4),
+                    rhs_scale=o2_plane[:, g2, :],
+                    start=(g2 == 0),
+                    stop=(g2 == 7),
+                )
+
+        def fin(grp):
+            j0, cnt = W2_GROUPS[grp]
+            for j in range(j0, j0 + cnt):
                 nc.vector.tensor_tensor(
-                    out=out_sb[:, hh, :, j, :],
+                    out=out_sb[:, :, j, :],
                     in0=accs[j][:, 0:P].rearrange("o (b s) -> o b s", b=2),
-                    in1=resb[:, 8 * hh + j, :].rearrange("o (b s) -> o b s", b=2),
+                    in1=resb[:, j, :].rearrange("o (b s) -> o b s", b=2),
                     op=ALU.add,
                 )
             for b in range(2):
                 nc.sync.dma_start(
-                    out=out[b, 1024 * hh : 1024 * hh + 1024].rearrange("(j o) h w -> o j (h w)", o=P),
-                    in_=out_sb[:, hh, b],
+                    out=out[b, P * j0 : P * (j0 + cnt)].rearrange("(j o) h w -> o j (h w)", o=P),
+                    in_=out_sb[:, b, j0 : j0 + cnt, :],
                 )
+
+        for kg in range(4):
+            mm1(0, kg)
+        for kg in range(3):
+            mm1(1, kg)
+        act(0)
+        act(1)
+        tr(0)
+        mm1(1, 3)
+        act(2)
+        cq(0)
+        tr(1)
+        mm1(2, 0)
+        act(3)
+        cq(1)
+        tr(2)
+        mm1(2, 1)
+        act(4)
+        cq(2)
+        tr(3)
+        mm1(2, 2)
+        act(5)
+        cq(3)
+        tr(4)
+        mm1(2, 3)
+        act(6)
+        cq(4)
+        tr(5)
+        mm2(0, 0)
+        act(7)
+        cq(5)
+        tr(6)
+        mm2(0, 1)
+        cq(6)
+        tr(7)
+        mm2(0, 2)
+        cq(7)
+        for g2 in range(3, 8):
+            mm2(0, g2)
+        fin(0)
+        for g2 in range(8):
+            mm2(1, g2)
+        fin(1)
+        for g2 in range(8):
+            mm2(2, g2)
+        fin(2)

@@ -212,18 +212,20 @@ def tile_memoryefficientpatchdownscale_w_kernel(
 
         def fin(grp):
             j0, cnt = W2_GROUPS[grp]
-            for j in range(j0, j0 + cnt):
-                nc.vector.tensor_tensor(
-                    out=out_sb[:, :, j, :],
-                    in0=accs[j][:, 0:P].rearrange("o (b s) -> o b s", b=2),
-                    in1=resb[:, j, :].rearrange("o (b s) -> o b s", b=2),
-                    op=ALU.add,
-                )
-            for b in range(2):
-                nc.sync.dma_start(
-                    out=out[b, P * j0 : P * (j0 + cnt)].rearrange("(j o) h w -> o j (h w)", o=P),
-                    in_=out_sb[:, b, j0 : j0 + cnt, :],
-                )
+            step = (cnt + 1) // 2 if cnt > 4 else cnt
+            for ja in range(j0, j0 + cnt, step):
+                for j in range(ja, ja + step):
+                    nc.vector.tensor_tensor(
+                        out=out_sb[:, :, j, :],
+                        in0=accs[j][:, 0:P].rearrange("o (b s) -> o b s", b=2),
+                        in1=resb[:, j, :].rearrange("o (b s) -> o b s", b=2),
+                        op=ALU.add,
+                    )
+                for b in range(2):
+                    nc.sync.dma_start(
+                        out=out[b, P * ja : P * (ja + step)].rearrange("(j o) h w -> o j (h w)", o=P),
+                        in_=out_sb[:, b, ja : ja + step, :],
+                    )
 
         for kg in range(4):
             mm1(0, kg)

@@ -18,8 +18,7 @@ OC = 2048
 K1 = 2048
 FLOPS = 2 * P * K1 * HID + 2 * P * HID * OC
 
-W1_CHUNKS = ((0, 2048), (2048, 1024), (3072, 1024))
-W2_GROUPS = ((0, 6), (6, 8), (14, 2))
+N = 512
 
 
 def tile_memoryefficientpatchdownscale_w_kernel(
@@ -29,21 +28,23 @@ def tile_memoryefficientpatchdownscale_w_kernel(
     with ExitStack() as ctx:
         keep = ctx.enter_context(tc.tile_pool(name="keep", bufs=1))
         work = ctx.enter_context(tc.tile_pool(name="work", bufs=4))
-        psum = ctx.enter_context(tc.psum_pool(name="psum", bufs=8))
+        psum = ctx.enter_context(tc.psum_pool(name="psum", bufs=1))
         ctx.enter_context(tc.manual_schedule())
 
-        b1rows = keep.tile([P, 512], BF16, name="b1rows")
-        b2rows = keep.tile([P, P], BF16, name="b2rows")
+        def bank(k, name):
+            return psum.tile([P, N], F32, name=name, tag="b%d" % k)
+
         s1 = keep.tile([P, HID], U8, name="s1", align_bytes=64)
         s2 = keep.tile([P, 2, OC], U8, name="s2", align_bytes=64)
+        b1rows = keep.tile([P, N], BF16, name="b1rows")
+        b2rows = keep.tile([P, N], BF16, name="b2rows")
         warm = keep.tile([P, 1], F32, name="warm")
+        warm2 = keep.tile([P, 1], F32, name="warm2")
+        nc.vector.memset(warm[:], 0.0)
         nc.vector.memset(b1rows[:], 0.0)
         nc.vector.memset(b2rows[:], 0.0)
         nc.vector.memset(s1[:].bitcast(I32), 0)
         nc.vector.memset(s2[:].bitcast(I32), 0)
-        nc.vector.memset(warm[:], 0.0)
-
-        warm2 = keep.tile([P, 1], F32, name="warm2")
         nc.scalar.activation(out=warm2[:], in_=warm[:], func=ACT.Silu)
 
         ident = keep.tile([P, P], BF16, name="ident")
@@ -64,104 +65,113 @@ def tile_memoryefficientpatchdownscale_w_kernel(
         x_dst = x_sb[:].rearrange("p (g b i) u j v -> p g b (i u j v)", g=4, b=2)
         for b in range(2):
             nc.sync.dma_start(out=x_dst[:, :, b, :], in_=x[b].rearrange("(g p) h w -> p g (h w)", p=P))
-        nc.sync.dma_start(out=b2rows[0:16, :], in_=bias2.rearrange("(j o) -> j o", o=P))
-        nc.sync.dma_start(out=b1rows[0:8, :], in_=bias1.rearrange("(g f) -> g f", f=512))
+        nc.sync.dma_start(out=b1rows[0:8, :], in_=bias1.rearrange("(g f) -> g f", f=N))
+        nc.sync.dma_start(out=b2rows[0:4, :], in_=bias2.rearrange("(g f) -> g f", f=N))
         w1t = {}
-        for c, (col0, width) in enumerate(W1_CHUNKS):
-            for kg in range(4):
-                t = keep.tile([P, width], U32, name="w1_%d_%d" % (c, kg), align_bytes=64)
-                src = weight1_words[kg].rearrange("p n t -> p (n t)")[:, 4 * col0 : 4 * (col0 + width)]
-                nc.sync.dma_start(out=t[:].bitcast(I32), in_=src.bitcast(I32))
-                w1t[(c, kg)] = t
-        w2t = {}
-        for grp in range(2):
-            j0, cnt = W2_GROUPS[grp]
-            for g2 in range(8):
-                t = keep.tile([P, P * cnt], U32, name="w2_%d_%d" % (grp, g2), align_bytes=64)
-                src = weight2_words[g2].rearrange("p n t -> p (n t)")[:, 4 * P * j0 : 4 * P * (j0 + cnt)]
-                nc.sync.dma_start(out=t[:].bitcast(I32), in_=src.bitcast(I32))
-                w2t[(grp, g2)] = t[:]
-        j0, cnt = W2_GROUPS[2]
         for h in range(2):
-            t = keep.tile([P, 4, P * cnt], U32, name="w2_2_%d" % h, align_bytes=64)
-            src = weight2_words[4 * h : 4 * h + 4].rearrange("g p n t -> p g (n t)")
-            nc.sync.dma_start(out=t[:].bitcast(I32), in_=src[:, :, 4 * P * j0 : 4 * P * (j0 + cnt)].bitcast(I32))
-            for gl in range(4):
-                w2t[(2, 4 * h + gl)] = t[:, gl, :]
+            for kg in range(4):
+                t = keep.tile([P, HID // 2], U32, name="w1_%d_%d" % (h, kg), align_bytes=64)
+                src = weight1_words[kg].rearrange("p n t -> p (n t)")[:, 2 * HID * h : 2 * HID * (h + 1)]
+                nc.sync.dma_start(out=t[:].bitcast(I32), in_=src.bitcast(I32))
+                w1t[(h, kg)] = t
+        w2t = {}
 
-        rsel = keep.tile([P, P, 4], BF16, name="rsel")
-        nc.vector.tensor_scalar_mul(out=rsel[:], in0=ident[:].unsqueeze(2).to_broadcast([P, P, 4]), scalar1=0.25)
-        rflat = rsel[:].rearrange("c q r -> c (q r)")
+        def load_w2(g0, cnt, c0, width):
+            t = keep.tile([P, cnt, N * width], U32, name="w2_%d_%d" % (g0, c0), align_bytes=64)
+            src = weight2_words[g0 : g0 + cnt].rearrange("g p n t -> p g (n t)")
+            nc.sync.dma_start(
+                out=t[:].bitcast(I32), in_=src[:, :, 4 * N * c0 : 4 * N * (c0 + width)].bitcast(I32)
+            )
+            for gl in range(cnt):
+                for cl in range(width):
+                    w2t[(g0 + gl, c0 + cl)] = t[:, gl, N * cl : N * cl + N]
+
+        for g2 in range(4):
+            load_w2(g2, 1, 0, 4)
+        load_w2(4, 2, 0, 2)
+        load_w2(6, 2, 0, 2)
+        load_w2(4, 2, 2, 1)
+        load_w2(6, 2, 2, 1)
+        load_w2(4, 2, 3, 1)
+        load_w2(6, 1, 3, 1)
+        load_w2(7, 1, 3, 1)
+
         grouped = keep.tile([P, 64, 8, 2, 2], BF16, name="grouped", align_bytes=64)
         nc.vector.tensor_copy(
             out=grouped[:].bitcast(F32)[:, :, :, :, 0],
             in_=x_sb[:].bitcast(F32)[:, :, :, :, 0].rearrange("p s u j -> p s j u"),
         )
-        p_codes = keep.tile([P, 512], U32, name="p_codes", align_bytes=64)
-        p_plane = keep.tile([P, 512], U8, name="p_plane", align_bytes=64)
+        p_codes = keep.tile([P, N], U32, name="p_codes", align_bytes=64)
+        p_plane = keep.tile([P, N], U8, name="p_plane", align_bytes=64)
         nc.vector.quantize_mx(
             out=p_codes[:].bitcast(FP8X4),
             scales=p_plane[:],
             in_=grouped[:].rearrange("p s j u v -> p (s j u v)"),
         )
 
-        resb = keep.tile([P, 16, P], F32, name="resb")
-        res_ps = []
-        for a in range(4):
-            ps = psum.tile([P, 512], F32, name="ps_res", tag="bank")
-            for n in range(4):
-                nc.tensor.matmul(
-                    out=ps[:].rearrange("o (s j) -> o s j", j=8),
-                    lhsT=rflat[:, P * a : P * a + P],
-                    rhs=x_sb[:, :, n // 2, :, n % 2],
-                    start=(n == 0),
-                    stop=(n == 3),
-                )
-            res_ps.append(ps)
-
-        ps_b2 = psum.tile([P, 512], F32, name="ps_b2", tag="bank")
-        nc.tensor.transpose(ps_b2[:].bitcast(BF16)[:, 0:P], b2rows[:], ident[:])
-        b2col = keep.tile([P, 16], F32, name="b2col")
-        nc.vector.tensor_copy(out=b2col[:], in_=ps_b2[:].bitcast(BF16)[:, 0:16])
-
-        for a in range(4):
-            nc.vector.tensor_tensor(
-                out=resb[:, a:16:4, :],
-                in0=res_ps[a][:].rearrange("o (g r) -> o g r", g=4),
-                in1=b2col[:, a:16:4].unsqueeze(2).to_broadcast([P, 4, P]),
-                op=ALU.add,
-            )
-
         b1bc = keep.tile([P, 8, 4, P], BF16, name="b1bc")
         for g in range(8):
-            ps = psum.tile([P, 512], F32, name="ps_b1", tag="bank")
+            ps = bank(4 + g % 4, "ps_b1")
             nc.tensor.matmul(
                 out=ps[:], lhsT=ident[:, g : g + 1].to_broadcast([P, P]), rhs=b1rows[:], start=True, stop=True
             )
             nc.scalar.copy(out=b1bc[:, g], in_=ps[:].rearrange("m (p t) -> m t p", t=4))
 
+        ps_b2 = bank(0, "ps_b2")
+        for e in range(4):
+            nc.tensor.transpose(
+                ps_b2[:].bitcast(BF16)[:, P * e : P * e + P],
+                b2rows[:].rearrange("r (n e) -> r e n", e=4)[:, e, :],
+                ident[:],
+            )
+        b2col = keep.tile([P, 4, 4], F32, name="b2col")
+        nc.vector.tensor_copy(
+            out=b2col[:],
+            in_=ps_b2[:].bitcast(BF16)[:, 0 : 4 * P].rearrange("p (e r) -> p r e", e=4)[:, 0:4, :],
+        )
+
+        psum_uv = keep.tile([P, 64, 8, 2], F32, name="psum_uv")
+        nc.vector.tensor_tensor(out=psum_uv[:], in0=x_sb[:, :, 0], in1=x_sb[:, :, 1], op=ALU.add)
+        pooled = keep.tile([P, 4, P], F32, name="pooled")
+        nc.vector.tensor_tensor(
+            out=pooled[:].rearrange("p c (s j) -> p (c s) j", j=8),
+            in0=psum_uv[:, :, :, 0],
+            in1=psum_uv[:, :, :, 1],
+            op=ALU.add,
+        )
+        resb = keep.tile([P, 4, 4, P], F32, name="resb")
+        for c in range(4):
+            nc.vector.scalar_tensor_tensor(
+                out=resb[:, c],
+                in0=pooled[:, c, :].unsqueeze(1).to_broadcast([P, 4, P]),
+                scalar=0.25,
+                in1=b2col[:, c, :].unsqueeze(2).to_broadcast([P, 4, P]),
+                op0=ALU.mult,
+                op1=ALU.add,
+            )
+        identf = keep.tile([P, P], F32, name="identf")
+        nc.vector.tensor_copy(out=identf[:], in_=ident[:])
+
         og = keep.tile([P, 8, P, 4], BF16, name="og", align_bytes=64)
         o2_codes = keep.tile([P, 8, P], U32, name="o2_codes", align_bytes=64)
         o2_plane = keep.tile([P, 8, P], U8, name="o2_plane", align_bytes=64)
-        out_sb = keep.tile([P, 2, 16, 64], F32, name="out_sb")
+        out_sb = keep.tile([P, 4, 2, 4, 64], F32, name="out_sb")
         banks = {}
         o2s = {}
         pts = {}
         accs = {}
 
-        def mm1(c, kg):
-            col0, width = W1_CHUNKS[c]
-            for n in range(width // 512):
-                g2 = col0 // 512 + n
+        def mm1(h, kg):
+            for n in range(4):
+                g2 = 4 * h + n
                 if kg == 0:
-                    bank = psum.tile([P, 512], F32, name="ps_o1", tag="bank")
-                    banks[g2] = bank
+                    banks[g2] = bank(g2, "ps_o1")
                 nc.tensor.matmul_mx(
                     out=banks[g2][:],
                     lhsT=p_codes[:, P * kg : P * kg + P].bitcast(FP8X4),
                     lhsT_scale=p_plane[:, P * kg : P * kg + P],
-                    rhs=w1t[(c, kg)][:, 512 * n : 512 * n + 512].bitcast(FP8X4),
-                    rhs_scale=s1[4 * kg : P, 512 * g2 : 512 * g2 + 512],
+                    rhs=w1t[(h, kg)][:, N * n : N * n + N].bitcast(FP8X4),
+                    rhs_scale=s1[4 * kg : P, N * g2 : N * g2 + N],
                     start=(kg == 0),
                     stop=(kg == 3),
                 )
@@ -176,99 +186,77 @@ def tile_memoryefficientpatchdownscale_w_kernel(
             o2s[g2] = o2
 
         def tr(g2):
-            pt = psum.tile([P, 512], F32, name="ps_t", tag="bank")
+            pt = bank(g2 % 4, "ps_t")
             for t in range(4):
                 nc.tensor.transpose(pt[:].bitcast(BF16)[:, P * t : P * t + P], o2s[g2][:, t, :], ident[:])
             pts[g2] = pt
 
         def cq(g2):
-            src = pts[g2][:].bitcast(BF16)[:, 0:512].rearrange("p (t r) -> p r t", t=4)
-            if g2 % 3 == 2:
-                nc.vector.tensor_copy(out=og[:, g2], in_=src)
-            else:
-                nc.scalar.copy(out=og[:, g2], in_=src)
+            nc.scalar.copy(
+                out=og[:, g2], in_=pts[g2][:].bitcast(BF16)[:, 0:N].rearrange("p (t r) -> p r t", t=4)
+            )
             nc.vector.quantize_mx(
                 out=o2_codes[:, g2, :].bitcast(FP8X4),
                 scales=o2_plane[:, g2, :],
                 in_=og[:, g2].rearrange("p r t -> p (r t)"),
             )
 
-        def mm2(grp, g2):
-            j0, cnt = W2_GROUPS[grp]
-            for jj in range(cnt):
-                j = j0 + jj
-                if g2 == 0:
-                    acc = psum.tile([P, 512], F32, name="ps_o3", tag="bank")
-                    accs[j] = acc
-                nc.tensor.matmul_mx(
-                    out=accs[j][:, 0:P],
-                    lhsT=w2t[(grp, g2)][:, P * jj : P * jj + P].bitcast(FP8X4),
-                    lhsT_scale=s2[4 * (g2 % 4) : P, g2 // 4, P * j : P * j + P],
-                    rhs=o2_codes[:, g2, :].bitcast(FP8X4),
-                    rhs_scale=o2_plane[:, g2, :],
-                    start=(g2 == 0),
-                    stop=(g2 == 7),
-                )
+        def mm2(g2, c):
+            if g2 == 0:
+                accs[c] = bank(4 + c, "ps_o3")
+            nc.tensor.matmul_mx(
+                out=accs[c][:],
+                lhsT=o2_codes[:, g2, :].bitcast(FP8X4),
+                lhsT_scale=o2_plane[:, g2, :],
+                rhs=w2t[(g2, c)].bitcast(FP8X4),
+                rhs_scale=s2[4 * (g2 % 4) : P, g2 // 4, N * c : N * c + N],
+                start=(g2 == 0),
+                stop=(g2 == 7),
+            )
 
-        def fin(grp):
-            j0, cnt = W2_GROUPS[grp]
-            step = (cnt + 1) // 2 if cnt > 4 else cnt
-            for ja in range(j0, j0 + cnt, step):
-                for j in range(ja, ja + step):
-                    nc.vector.tensor_tensor(
-                        out=out_sb[:, :, j, :],
-                        in0=accs[j][:, 0:P].rearrange("o (b s) -> o b s", b=2),
-                        in1=resb[:, j, :].rearrange("o (b s) -> o b s", b=2),
-                        op=ALU.add,
-                    )
-                for b in range(2):
-                    nc.sync.dma_start(
-                        out=out[b, P * ja : P * (ja + step)].rearrange("(j o) h w -> o j (h w)", o=P),
-                        in_=out_sb[:, b, ja : ja + step, :],
-                    )
+        def fin(c):
+            o3 = work.tile([P, 4, P], F32, name="o3")
+            nc.scalar.copy(out=o3[:], in_=accs[c][:].rearrange("m (n e) -> m e n", e=4))
+            pt = bank(c, "ps_f")
+            for e in range(4):
+                nc.tensor.transpose(pt[:, P * e : P * e + P], o3[:, e, :], identf[:])
+            nc.vector.tensor_tensor(
+                out=out_sb[:, c].rearrange("p b e s -> p e b s"),
+                in0=pt[:].rearrange("p (e b s) -> p e b s", e=4, b=2),
+                in1=resb[:, c].rearrange("p e (b s) -> p e b s", b=2),
+                op=ALU.add,
+            )
+            nc.sync.dma_start(
+                out=out[:, N * c : N * c + N].rearrange("b (p e) h w -> p b (e h w)", e=4),
+                in_=out_sb[:, c].rearrange("p b e s -> p b (e s)"),
+            )
 
         for kg in range(4):
             mm1(0, kg)
-        for kg in range(3):
+        for g2 in range(4):
+            act(g2)
+        mm1(1, 0)
+        for g2 in range(4):
+            tr(g2)
+            cq(g2)
+        for kg in range(1, 4):
             mm1(1, kg)
-        act(0)
-        act(1)
-        tr(0)
-        mm1(1, 3)
-        act(2)
-        cq(0)
-        tr(1)
-        mm1(2, 0)
-        act(3)
-        cq(1)
-        tr(2)
-        mm1(2, 1)
-        act(4)
-        cq(2)
-        tr(3)
-        mm1(2, 2)
-        act(5)
-        cq(3)
-        tr(4)
-        mm1(2, 3)
-        act(6)
-        cq(4)
-        tr(5)
-        mm2(0, 0)
-        act(7)
-        cq(5)
-        tr(6)
-        mm2(0, 1)
-        cq(6)
-        tr(7)
-        mm2(0, 2)
-        cq(7)
-        for g2 in range(3, 8):
-            mm2(0, g2)
-        fin(0)
-        for g2 in range(8):
-            mm2(1, g2)
-        fin(1)
-        for g2 in range(8):
-            mm2(2, g2)
-        fin(2)
+        for g2 in range(4, 8):
+            act(g2)
+        for c in range(4):
+            mm2(0, c)
+        for g2 in range(4, 8):
+            tr(g2)
+            cq(g2)
+        for g2 in range(1, 4):
+            for c in range(4):
+                mm2(g2, c)
+        for g2 in range(4, 8):
+            for c in range(2):
+                mm2(g2, c)
+        for c in range(2):
+            fin(c)
+        for c in range(2, 4):
+            for g2 in range(4, 8):
+                mm2(g2, c)
+            fin(c)

@@ -40,20 +40,16 @@ def tile_memoryefficientpatchdownscale_w_kernel(
         b2rows = keep.tile([P, N], BF16, name="b2rows")
         warm = keep.tile([P, 1], F32, name="warm")
         warm2 = keep.tile([P, 1], F32, name="warm2")
-        nc.vector.memset(warm[:], 0.0)
+        nc.vector.memset(s1[:, 0 : HID // 2].bitcast(I32), 0)
+        nc.gpsimd.memset(s1[:, HID // 2 : HID].bitcast(I32), 0)
         nc.vector.memset(b1rows[:], 0.0)
         nc.vector.memset(b2rows[:], 0.0)
-        nc.vector.memset(s1[:].bitcast(I32), 0)
+        nc.vector.memset(warm[:], 0.0)
         nc.vector.memset(s2[:].bitcast(I32), 0)
         nc.scalar.activation(out=warm2[:], in_=warm[:], func=ACT.Silu)
 
         ident = keep.tile([P, P], BF16, name="ident")
         make_identity(nc, ident[:])
-        for q in range(4):
-            nc.gpsimd.dma_start(
-                out=s1[32 * q : 32 * q + 16, :].bitcast(F32),
-                in_=weight1_scales[:, 4 * q : 4 * q + 4, :].bitcast(F32),
-            )
         for h in range(2):
             for q in range(4):
                 nc.gpsimd.dma_start(
@@ -65,6 +61,11 @@ def tile_memoryefficientpatchdownscale_w_kernel(
         x_dst = x_sb[:].rearrange("p (g b i) u j v -> p g b (i u j v)", g=4, b=2)
         for b in range(2):
             nc.sync.dma_start(out=x_dst[:, :, b, :], in_=x[b].rearrange("(g p) h w -> p g (h w)", p=P))
+        for q in range(4):
+            nc.sync.dma_start(
+                out=s1[32 * q : 32 * q + 16, :].bitcast(I32),
+                in_=weight1_scales[:, 4 * q : 4 * q + 4, :].bitcast(I32),
+            )
         nc.sync.dma_start(out=b1rows[0:8, :], in_=bias1.rearrange("(g f) -> g f", f=N))
         nc.sync.dma_start(out=b2rows[0:4, :], in_=bias2.rearrange("(g f) -> g f", f=N))
         w1t = {}

@@ -48,6 +48,20 @@ def tile_memoryefficientpatchdownscale_w_kernel(
         nc.vector.memset(s2[:].bitcast(I32), 0)
         nc.scalar.activation(out=warm2[:], in_=warm[:], func=ACT.Silu)
 
+        w1t = {}
+        for h in range(2):
+            for kg in range(4):
+                w1t[(h, kg)] = keep.tile([P, HID // 2], U32, name="w1_%d_%d" % (h, kg), align_bytes=64)
+
+        def gate(h, kg):
+            nc.gpsimd.memset(w1t[(h, kg)][:, 0:16].bitcast(I32), 0)
+
+        for q in range(4):
+            nc.gpsimd.dma_start(
+                out=s1[32 * q : 32 * q + 16, :].bitcast(F32),
+                in_=weight1_scales[:, 4 * q : 4 * q + 4, :].bitcast(F32),
+            )
+        gate(0, 3)
         ident = keep.tile([P, P], BF16, name="ident")
         make_identity(nc, ident[:])
         for h in range(2):
@@ -56,25 +70,18 @@ def tile_memoryefficientpatchdownscale_w_kernel(
                     out=s2[32 * q : 32 * q + 16, h, :].bitcast(F32),
                     in_=weight2_scales[4 * h : 4 * h + 4, 4 * q : 4 * q + 4, :].bitcast(F32),
                 )
+            gate(1, 1 + 2 * h)
 
         x_sb = keep.tile([P, 64, 2, 8, 2], BF16, name="x_sb", align_bytes=64)
         x_dst = x_sb[:].rearrange("p (g b i) u j v -> p g b (i u j v)", g=4, b=2)
         for b in range(2):
             nc.sync.dma_start(out=x_dst[:, :, b, :], in_=x[b].rearrange("(g p) h w -> p g (h w)", p=P))
-        for q in range(4):
-            nc.sync.dma_start(
-                out=s1[32 * q : 32 * q + 16, :].bitcast(I32),
-                in_=weight1_scales[:, 4 * q : 4 * q + 4, :].bitcast(I32),
-            )
         nc.sync.dma_start(out=b1rows[0:8, :], in_=bias1.rearrange("(g f) -> g f", f=N))
         nc.sync.dma_start(out=b2rows[0:4, :], in_=bias2.rearrange("(g f) -> g f", f=N))
-        w1t = {}
         for h in range(2):
             for kg in range(4):
-                t = keep.tile([P, HID // 2], U32, name="w1_%d_%d" % (h, kg), align_bytes=64)
                 src = weight1_words[kg].rearrange("p n t -> p (n t)")[:, 2 * HID * h : 2 * HID * (h + 1)]
-                nc.sync.dma_start(out=t[:].bitcast(I32), in_=src.bitcast(I32))
-                w1t[(h, kg)] = t
+                nc.sync.dma_start(out=w1t[(h, kg)][:].bitcast(I32), in_=src.bitcast(I32))
         w2t = {}
 
         def load_w2(g0, cnt, c0, width):
@@ -161,6 +168,7 @@ def tile_memoryefficientpatchdownscale_w_kernel(
         o2s = {}
         pts = {}
         accs = {}
+        o3s = {}
 
         def mm1(h, kg):
             for n in range(4):
@@ -187,7 +195,7 @@ def tile_memoryefficientpatchdownscale_w_kernel(
             o2s[g2] = o2
 
         def tr(g2):
-            pt = bank(g2 % 4, "ps_t")
+            pt = bank(g2 % 4 if g2 < 4 else g2 % 3, "ps_t")
             for t in range(4):
                 nc.tensor.transpose(pt[:].bitcast(BF16)[:, P * t : P * t + P], o2s[g2][:, t, :], ident[:])
             pts[g2] = pt
@@ -215,9 +223,12 @@ def tile_memoryefficientpatchdownscale_w_kernel(
                 stop=(g2 == 7),
             )
 
+        def evac(c):
+            o3s[c] = work.tile([P, 4, P], F32, name="o3")
+            nc.scalar.copy(out=o3s[c][:], in_=accs[c][:].rearrange("m (n e) -> m e n", e=4))
+
         def fin(c):
-            o3 = work.tile([P, 4, P], F32, name="o3")
-            nc.scalar.copy(out=o3[:], in_=accs[c][:].rearrange("m (n e) -> m e n", e=4))
+            o3 = o3s[c]
             pt = bank(c, "ps_f")
             for e in range(4):
                 nc.tensor.transpose(pt[:, P * e : P * e + P], o3[:, e, :], identf[:])
@@ -232,6 +243,40 @@ def tile_memoryefficientpatchdownscale_w_kernel(
                 in_=out_sb[:, c].rearrange("p b e s -> p b (e s)"),
             )
 
+        def mm2_half(g2, half):
+            if g2 == 0:
+                accs[3 + half] = bank((7, 3)[half], "ps_o3")
+            cols = slice(256 * half, 256 * half + 256)
+            nc.tensor.matmul_mx(
+                out=accs[3 + half][:, 0:256],
+                lhsT=o2_codes[:, g2, :].bitcast(FP8X4),
+                lhsT_scale=o2_plane[:, g2, :],
+                rhs=w2t[(g2, 3)][:, cols].bitcast(FP8X4),
+                rhs_scale=s2[4 * (g2 % 4) : P, g2 // 4, 3 * N + 256 * half : 3 * N + 256 * half + 256],
+                start=(g2 == 0),
+                stop=(g2 == 7),
+            )
+
+        def last_fin():
+            o3 = work.tile([P, 4, P], F32, name="o3")
+            nc.scalar.copy(out=o3[:, :, 0:64], in_=accs[3][:, 0:256].rearrange("m (n e) -> m e n", e=4))
+            nc.vector.tensor_copy(out=o3[:, :, 64:P], in_=accs[4][:, 0:256].rearrange("m (n e) -> m e n", e=4))
+            for k in range(2):
+                pt = bank(k, "ps_f")
+                for e in range(2):
+                    nc.tensor.transpose(pt[:, P * e : P * e + P], o3[:, 2 * k + e, :], identf[:])
+                nc.vector.tensor_tensor(
+                    out=out_sb[:, 3, :, 2 * k : 2 * k + 2, :].rearrange("p b e s -> p e b s"),
+                    in0=pt[:, 0 : 2 * P].rearrange("p (e b s) -> p e b s", e=2, b=2),
+                    in1=resb[:, 3, 2 * k : 2 * k + 2, :].rearrange("p e (b s) -> p e b s", b=2),
+                    op=ALU.add,
+                )
+                nc.sync.dma_start(
+                    out=out[:, 3 * N : 4 * N].rearrange("b (p e) h w -> p b e (h w)", e=4)[:, :, 2 * k : 2 * k + 2, :]
+                    .rearrange("p b e s -> p b (e s)"),
+                    in_=out_sb[:, 3, :, 2 * k : 2 * k + 2, :].rearrange("p b e s -> p b (e s)"),
+                )
+
         for kg in range(4):
             mm1(0, kg)
         for g2 in range(4):
@@ -244,20 +289,37 @@ def tile_memoryefficientpatchdownscale_w_kernel(
             mm1(1, kg)
         for g2 in range(4, 8):
             act(g2)
-        for c in range(4):
-            mm2(0, c)
+        def mm2_all(g2):
+            for c in range(3):
+                mm2(g2, c)
+            for half in range(2):
+                mm2_half(g2, half)
+
+        mm2_all(0)
         for g2 in range(4, 8):
             tr(g2)
             cq(g2)
         for g2 in range(1, 4):
-            for c in range(4):
-                mm2(g2, c)
-        for g2 in range(4, 8):
+            mm2_all(g2)
+        for g2 in range(4, 6):
             for c in range(2):
                 mm2(g2, c)
         for c in range(2):
-            fin(c)
-        for c in range(2, 4):
-            for g2 in range(4, 8):
+            for g2 in range(6, 8):
                 mm2(g2, c)
-            fin(c)
+            evac(c)
+        mm2(4, 2)
+        mm2(5, 2)
+        fin(0)
+        fin(1)
+        mm2(6, 2)
+        mm2(7, 2)
+        evac(2)
+        for g2 in range(4, 6):
+            for half in range(2):
+                mm2_half(g2, half)
+        fin(2)
+        for g2 in range(6, 8):
+            for half in range(2):
+                mm2_half(g2, half)
+        last_fin()

@@ -40,11 +40,15 @@ def tile_memoryefficientpatchdownscale_w_kernel(
         b2rows = keep.tile([P, N], BF16, name="b2rows")
         warm = keep.tile([P, 1], F32, name="warm")
         warm2 = keep.tile([P, 1], F32, name="warm2")
-        nc.vector.memset(s1[:, 0 : HID // 2].bitcast(I32), 0)
-        nc.gpsimd.memset(s1[:, HID // 2 : HID].bitcast(I32), 0)
+        ident = keep.tile([P, P], BF16, name="ident")
+        make_identity(nc, ident[:])
+        nc.vector.memset(s1[:].bitcast(I32), 0)
         nc.vector.memset(b1rows[:], 0.0)
         nc.vector.memset(b2rows[:], 0.0)
         nc.vector.memset(warm[:], 0.0)
+        rsel = keep.tile([P, P, 4], BF16, name="rsel")
+        nc.vector.tensor_scalar_mul(out=rsel[:], in0=ident[:].unsqueeze(2).to_broadcast([P, P, 4]), scalar1=0.25)
+        rflat = rsel[:].rearrange("c q r -> c (q r)")
         nc.vector.memset(s2[:].bitcast(I32), 0)
         nc.scalar.activation(out=warm2[:], in_=warm[:], func=ACT.Silu)
 
@@ -62,8 +66,6 @@ def tile_memoryefficientpatchdownscale_w_kernel(
                 in_=weight1_scales[:, 4 * q : 4 * q + 4, :].bitcast(F32),
             )
         gate(0, 3)
-        ident = keep.tile([P, P], BF16, name="ident")
-        make_identity(nc, ident[:])
         for h in range(2):
             for q in range(4):
                 nc.gpsimd.dma_start(
@@ -94,15 +96,27 @@ def tile_memoryefficientpatchdownscale_w_kernel(
                 for cl in range(width):
                     w2t[(g0 + gl, c0 + cl)] = t[:, gl, N * cl : N * cl + N]
 
+        def load_tiles(g0, cnt, j0):
+            t = keep.tile([P, cnt, 2 * P], U32, name="w2t_%d_%d" % (g0, j0), align_bytes=64)
+            src = weight2_words[g0 : g0 + cnt].rearrange("g p n t -> p g (n t)")
+            col0 = 3 * N + P * j0
+            nc.sync.dma_start(out=t[:].bitcast(I32), in_=src[:, :, 4 * col0 : 4 * (col0 + 2 * P)].bitcast(I32))
+            for gl in range(cnt):
+                for jl in range(2):
+                    w2j[(g0 + gl, j0 + jl)] = t[:, gl, P * jl : P * jl + P]
+
+        w2j = {}
         for g2 in range(4):
             load_w2(g2, 1, 0, 4)
+            for j in range(4):
+                w2j[(g2, j)] = w2t[(g2, 3)][:, P * j : P * j + P]
         load_w2(4, 2, 0, 2)
         load_w2(6, 2, 0, 2)
         load_w2(4, 2, 2, 1)
         load_w2(6, 2, 2, 1)
-        load_w2(4, 2, 3, 1)
-        load_w2(6, 1, 3, 1)
-        load_w2(7, 1, 3, 1)
+        load_tiles(4, 4, 0)
+        load_tiles(4, 2, 2)
+        load_tiles(6, 2, 2)
 
         grouped = keep.tile([P, 64, 8, 2, 2], BF16, name="grouped", align_bytes=64)
         nc.vector.tensor_copy(
@@ -138,6 +152,30 @@ def tile_memoryefficientpatchdownscale_w_kernel(
             in_=ps_b2[:].bitcast(BF16)[:, 0 : 4 * P].rearrange("p (e r) -> p r e", e=4)[:, 0:4, :],
         )
 
+        ps_b2t = bank(1, "ps_b2")
+        for j in range(4):
+            nc.tensor.transpose(ps_b2t[:].bitcast(BF16)[:, P * j : P * j + P], b2rows[:, P * j : P * j + P], ident[:])
+        b2t = keep.tile([P, 4], F32, name="b2t")
+        nc.vector.tensor_copy(
+            out=b2t[:], in_=ps_b2t[:].bitcast(BF16)[:, 0 : 4 * P].rearrange("p (j r) -> p r j", j=4)[:, 3, :]
+        )
+        resb_t = keep.tile([P, 4, P], F32, name="resb_t")
+        ps_res = bank(2, "ps_res")
+        for j in range(4):
+            for n in range(4):
+                nc.tensor.matmul(
+                    out=ps_res[:, P * j : P * j + P].rearrange("o (s j) -> o s j", j=8),
+                    lhsT=rflat[:, P * j : P * j + P],
+                    rhs=x_sb[:, 48:64, n // 2, :, n % 2],
+                    start=(n == 0),
+                    stop=(n == 3),
+                )
+        nc.vector.tensor_tensor(
+            out=resb_t[:],
+            in0=ps_res[:].rearrange("o (j t) -> o j t", j=4),
+            in1=b2t[:].unsqueeze(2).to_broadcast([P, 4, P]),
+            op=ALU.add,
+        )
         psum_uv = keep.tile([P, 64, 8, 2], F32, name="psum_uv")
         nc.vector.tensor_tensor(out=psum_uv[:], in0=x_sb[:, :, 0], in1=x_sb[:, :, 1], op=ALU.add)
         pooled = keep.tile([P, 4, P], F32, name="pooled")
@@ -147,8 +185,8 @@ def tile_memoryefficientpatchdownscale_w_kernel(
             in1=psum_uv[:, :, :, 1],
             op=ALU.add,
         )
-        resb = keep.tile([P, 4, 4, P], F32, name="resb")
-        for c in range(4):
+        resb = keep.tile([P, 3, 4, P], F32, name="resb")
+        for c in range(3):
             nc.vector.scalar_tensor_tensor(
                 out=resb[:, c],
                 in0=pooled[:, c, :].unsqueeze(1).to_broadcast([P, 4, P]),
@@ -163,7 +201,8 @@ def tile_memoryefficientpatchdownscale_w_kernel(
         og = keep.tile([P, 8, P, 4], BF16, name="og", align_bytes=64)
         o2_codes = keep.tile([P, 8, P], U32, name="o2_codes", align_bytes=64)
         o2_plane = keep.tile([P, 8, P], U8, name="o2_plane", align_bytes=64)
-        out_sb = keep.tile([P, 4, 2, 4, 64], F32, name="out_sb")
+        out_sb = keep.tile([P, 3, 2, 4, 64], F32, name="out_sb")
+        out_t = keep.tile([P, 4, P], F32, name="out_t")
         banks = {}
         o2s = {}
         pts = {}
@@ -243,39 +282,27 @@ def tile_memoryefficientpatchdownscale_w_kernel(
                 in_=out_sb[:, c].rearrange("p b e s -> p b (e s)"),
             )
 
-        def mm2_half(g2, half):
+        def mm2_tile(g2, j):
             if g2 == 0:
-                accs[3 + half] = bank((7, 3)[half], "ps_o3")
-            cols = slice(256 * half, 256 * half + 256)
+                accs[4 + j] = bank((7, 5, 3, 4)[j], "ps_o3")
+            col0 = 3 * N + P * j
             nc.tensor.matmul_mx(
-                out=accs[3 + half][:, 0:256],
-                lhsT=o2_codes[:, g2, :].bitcast(FP8X4),
-                lhsT_scale=o2_plane[:, g2, :],
-                rhs=w2t[(g2, 3)][:, cols].bitcast(FP8X4),
-                rhs_scale=s2[4 * (g2 % 4) : P, g2 // 4, 3 * N + 256 * half : 3 * N + 256 * half + 256],
+                out=accs[4 + j][:, 0:P],
+                lhsT=w2j[(g2, j)].bitcast(FP8X4),
+                lhsT_scale=s2[4 * (g2 % 4) : P, g2 // 4, col0 : col0 + P],
+                rhs=o2_codes[:, g2, :].bitcast(FP8X4),
+                rhs_scale=o2_plane[:, g2, :],
                 start=(g2 == 0),
                 stop=(g2 == 7),
             )
 
-        def last_fin():
-            o3 = work.tile([P, 4, P], F32, name="o3")
-            nc.scalar.copy(out=o3[:, :, 0:64], in_=accs[3][:, 0:256].rearrange("m (n e) -> m e n", e=4))
-            nc.vector.tensor_copy(out=o3[:, :, 64:P], in_=accs[4][:, 0:256].rearrange("m (n e) -> m e n", e=4))
-            for k in range(2):
-                pt = bank(k, "ps_f")
-                for e in range(2):
-                    nc.tensor.transpose(pt[:, P * e : P * e + P], o3[:, 2 * k + e, :], identf[:])
-                nc.vector.tensor_tensor(
-                    out=out_sb[:, 3, :, 2 * k : 2 * k + 2, :].rearrange("p b e s -> p e b s"),
-                    in0=pt[:, 0 : 2 * P].rearrange("p (e b s) -> p e b s", e=2, b=2),
-                    in1=resb[:, 3, 2 * k : 2 * k + 2, :].rearrange("p e (b s) -> p e b s", b=2),
-                    op=ALU.add,
-                )
-                nc.sync.dma_start(
-                    out=out[:, 3 * N : 4 * N].rearrange("b (p e) h w -> p b e (h w)", e=4)[:, :, 2 * k : 2 * k + 2, :]
-                    .rearrange("p b e s -> p b (e s)"),
-                    in_=out_sb[:, 3, :, 2 * k : 2 * k + 2, :].rearrange("p b e s -> p b (e s)"),
-                )
+        def fin_tile(j):
+            nc.vector.tensor_tensor(out=out_t[:, j, :], in0=accs[4 + j][:, 0:P], in1=resb_t[:, j, :], op=ALU.add)
+            col0 = 3 * N + P * j
+            nc.sync.dma_start(
+                out=out[:, col0 : col0 + P].rearrange("b o h w -> o b (h w)"),
+                in_=out_t[:, j, :].rearrange("o (b s) -> o b s", b=2),
+            )
 
         for kg in range(4):
             mm1(0, kg)
@@ -289,18 +316,17 @@ def tile_memoryefficientpatchdownscale_w_kernel(
             mm1(1, kg)
         for g2 in range(4, 8):
             act(g2)
-        def mm2_all(g2):
-            for c in range(3):
-                mm2(g2, c)
-            for half in range(2):
-                mm2_half(g2, half)
-
-        mm2_all(0)
+        for c in range(3):
+            mm2(0, c)
         for g2 in range(4, 8):
             tr(g2)
             cq(g2)
         for g2 in range(1, 4):
-            mm2_all(g2)
+            for c in range(3):
+                mm2(g2, c)
+        for j in (0, 2):
+            for g2 in range(4):
+                mm2_tile(g2, j)
         for g2 in range(4, 6):
             for c in range(2):
                 mm2(g2, c)
@@ -311,15 +337,23 @@ def tile_memoryefficientpatchdownscale_w_kernel(
         mm2(4, 2)
         mm2(5, 2)
         fin(0)
+        for g2 in range(4):
+            mm2_tile(g2, 3)
         fin(1)
+        for g2 in range(4):
+            mm2_tile(g2, 1)
         mm2(6, 2)
         mm2(7, 2)
         evac(2)
-        for g2 in range(4, 6):
-            for half in range(2):
-                mm2_half(g2, half)
+        for j in range(2):
+            for g2 in range(4, 8):
+                mm2_tile(g2, j)
+            fin_tile(j)
         fin(2)
-        for g2 in range(6, 8):
-            for half in range(2):
-                mm2_half(g2, half)
-        last_fin()
+        for g2 in range(4, 6):
+            for j in range(2, 4):
+                mm2_tile(g2, j)
+        for j in range(2, 4):
+            for g2 in range(6, 8):
+                mm2_tile(g2, j)
+            fin_tile(j)

@@ -78,12 +78,13 @@ def tile_memoryefficientpatchdownscale_w_kernel(
         x_dst = x_sb[:].rearrange("p (g b i) u j v -> p g b (i u j v)", g=4, b=2)
         for b in range(2):
             nc.sync.dma_start(out=x_dst[:, :, b, :], in_=x[b].rearrange("(g p) h w -> p g (h w)", p=P))
-        nc.sync.dma_start(out=b1rows[0:8, :], in_=bias1.rearrange("(g f) -> g f", f=N))
-        nc.sync.dma_start(out=b2rows[0:4, :], in_=bias2.rearrange("(g f) -> g f", f=N))
         for h in range(2):
             for kg in range(4):
                 src = weight1_words[kg].rearrange("p n t -> p (n t)")[:, 2 * HID * h : 2 * HID * (h + 1)]
                 nc.sync.dma_start(out=w1t[(h, kg)][:].bitcast(I32), in_=src.bitcast(I32))
+                if h == 0 and kg == 0:
+                    nc.sync.dma_start(out=b1rows[0:8, :], in_=bias1.rearrange("(g f) -> g f", f=N))
+                    nc.sync.dma_start(out=b2rows[0:4, :], in_=bias2.rearrange("(g f) -> g f", f=N))
         w2t = {}
 
         def load_w2(g0, cnt, c0, width):
@@ -96,27 +97,24 @@ def tile_memoryefficientpatchdownscale_w_kernel(
                 for cl in range(width):
                     w2t[(g0 + gl, c0 + cl)] = t[:, gl, N * cl : N * cl + N]
 
-        def load_tiles(g0, cnt, j0):
-            t = keep.tile([P, cnt, 2 * P], U32, name="w2t_%d_%d" % (g0, j0), align_bytes=64)
+        def load_tiles(g0, cnt, j0, tiles):
+            t = keep.tile([P, cnt, tiles * P], U32, name="w2t_%d_%d" % (g0, j0), align_bytes=64)
             src = weight2_words[g0 : g0 + cnt].rearrange("g p n t -> p g (n t)")
             col0 = 3 * N + P * j0
-            nc.sync.dma_start(out=t[:].bitcast(I32), in_=src[:, :, 4 * col0 : 4 * (col0 + 2 * P)].bitcast(I32))
+            nc.sync.dma_start(out=t[:].bitcast(I32), in_=src[:, :, 4 * col0 : 4 * (col0 + tiles * P)].bitcast(I32))
             for gl in range(cnt):
-                for jl in range(2):
+                for jl in range(tiles):
                     w2j[(g0 + gl, j0 + jl)] = t[:, gl, P * jl : P * jl + P]
 
         w2j = {}
-        for g2 in range(4):
-            load_w2(g2, 1, 0, 4)
-            for j in range(4):
-                w2j[(g2, j)] = w2t[(g2, 3)][:, P * j : P * j + P]
-        load_w2(4, 2, 0, 2)
-        load_w2(6, 2, 0, 2)
-        load_w2(4, 2, 2, 1)
-        load_w2(6, 2, 2, 1)
-        load_tiles(4, 4, 0)
-        load_tiles(4, 2, 2)
-        load_tiles(6, 2, 2)
+        for g2 in range(8):
+            load_w2(g2, 1, 0, 2)
+        for g2 in range(0, 8, 2):
+            load_w2(g2, 2, 2, 1)
+        load_tiles(0, 4, 0, 4)
+        load_tiles(4, 4, 0, 2)
+        load_tiles(4, 2, 2, 2)
+        load_tiles(6, 2, 2, 2)
 
         grouped = keep.tile([P, 64, 8, 2, 2], BF16, name="grouped", align_bytes=64)
         nc.vector.tensor_copy(
@@ -316,40 +314,35 @@ def tile_memoryefficientpatchdownscale_w_kernel(
             mm1(1, kg)
         for g2 in range(4, 8):
             act(g2)
-        for c in range(3):
+        for c in range(2):
             mm2(0, c)
         for g2 in range(4, 8):
             tr(g2)
             cq(g2)
-        for g2 in range(1, 4):
-            for c in range(3):
-                mm2(g2, c)
-        for j in (0, 2):
-            for g2 in range(4):
-                mm2_tile(g2, j)
-        for g2 in range(4, 6):
+        for g2 in range(1, 6):
             for c in range(2):
                 mm2(g2, c)
         for c in range(2):
             for g2 in range(6, 8):
                 mm2(g2, c)
             evac(c)
-        mm2(4, 2)
-        mm2(5, 2)
+        mm2(0, 2)
+        mm2(1, 2)
         fin(0)
-        for g2 in range(4):
-            mm2_tile(g2, 3)
+        mm2(2, 2)
+        mm2(3, 2)
         fin(1)
-        for g2 in range(4):
-            mm2_tile(g2, 1)
-        mm2(6, 2)
-        mm2(7, 2)
+        for g2 in range(4, 8):
+            mm2(g2, 2)
         evac(2)
+        fin(2)
+        for j in range(4):
+            for g2 in range(4):
+                mm2_tile(g2, j)
         for j in range(2):
             for g2 in range(4, 8):
                 mm2_tile(g2, j)
             fin_tile(j)
-        fin(2)
         for g2 in range(4, 6):
             for j in range(2, 4):
                 mm2_tile(g2, j)

@@ -57,22 +57,20 @@ def tile_memoryefficientpatchdownscale_w_kernel(
             for kg in range(4):
                 w1t[(h, kg)] = keep.tile([P, HID // 2], U32, name="w1_%d_%d" % (h, kg), align_bytes=64)
 
-        def gate(h, kg):
-            nc.gpsimd.memset(w1t[(h, kg)][:, 0:16].bitcast(I32), 0)
-
         for q in range(4):
             nc.gpsimd.dma_start(
                 out=s1[32 * q : 32 * q + 16, :].bitcast(F32),
                 in_=weight1_scales[:, 4 * q : 4 * q + 4, :].bitcast(F32),
             )
-        gate(0, 3)
+        nc.gpsimd.memset(w1t[(0, 3)][:, 0:16].bitcast(I32), 0)
         for h in range(2):
             for q in range(4):
                 nc.gpsimd.dma_start(
                     out=s2[32 * q : 32 * q + 16, h, :].bitcast(F32),
                     in_=weight2_scales[4 * h : 4 * h + 4, 4 * q : 4 * q + 4, :].bitcast(F32),
                 )
-            gate(1, 1 + 2 * h)
+        w2_first = keep.tile([P, 1, 3 * N], U32, name="w2_first", align_bytes=64)
+        nc.gpsimd.memset(w2_first[:, 0, 0:16].bitcast(I32), 0)
 
         x_sb = keep.tile([P, 64, 2, 8, 2], BF16, name="x_sb", align_bytes=64)
         x_dst = x_sb[:].rearrange("p (g b i) u j v -> p g b (i u j v)", g=4, b=2)
@@ -88,7 +86,10 @@ def tile_memoryefficientpatchdownscale_w_kernel(
         w2t = {}
 
         def load_w2(g0, cnt, c0, width):
-            t = keep.tile([P, cnt, N * width], U32, name="w2_%d_%d" % (g0, c0), align_bytes=64)
+            if g0 == 0:
+                t = w2_first
+            else:
+                t = keep.tile([P, cnt, N * width], U32, name="w2_%d_%d" % (g0, c0), align_bytes=64)
             src = weight2_words[g0 : g0 + cnt].rearrange("g p n t -> p g (n t)")
             nc.sync.dma_start(
                 out=t[:].bitcast(I32), in_=src[:, :, 4 * N * c0 : 4 * N * (c0 + width)].bitcast(I32)
@@ -108,12 +109,10 @@ def tile_memoryefficientpatchdownscale_w_kernel(
 
         w2j = {}
         for g2 in range(8):
-            load_w2(g2, 1, 0, 2)
-        for g2 in range(0, 8, 2):
-            load_w2(g2, 2, 2, 1)
+            load_w2(g2, 1, 0, 3)
         load_tiles(0, 4, 0, 4)
-        load_tiles(4, 4, 0, 2)
-        load_tiles(4, 2, 2, 2)
+        load_tiles(4, 2, 0, 4)
+        load_tiles(6, 2, 0, 2)
         load_tiles(6, 2, 2, 2)
 
         grouped = keep.tile([P, 64, 8, 2, 2], BF16, name="grouped", align_bytes=64)
@@ -174,25 +173,6 @@ def tile_memoryefficientpatchdownscale_w_kernel(
             in1=b2t[:].unsqueeze(2).to_broadcast([P, 4, P]),
             op=ALU.add,
         )
-        psum_uv = keep.tile([P, 64, 8, 2], F32, name="psum_uv")
-        nc.vector.tensor_tensor(out=psum_uv[:], in0=x_sb[:, :, 0], in1=x_sb[:, :, 1], op=ALU.add)
-        pooled = keep.tile([P, 4, P], F32, name="pooled")
-        nc.vector.tensor_tensor(
-            out=pooled[:].rearrange("p c (s j) -> p (c s) j", j=8),
-            in0=psum_uv[:, :, :, 0],
-            in1=psum_uv[:, :, :, 1],
-            op=ALU.add,
-        )
-        resb = keep.tile([P, 3, 4, P], F32, name="resb")
-        for c in range(3):
-            nc.vector.scalar_tensor_tensor(
-                out=resb[:, c],
-                in0=pooled[:, c, :].unsqueeze(1).to_broadcast([P, 4, P]),
-                scalar=0.25,
-                in1=b2col[:, c, :].unsqueeze(2).to_broadcast([P, 4, P]),
-                op0=ALU.mult,
-                op1=ALU.add,
-            )
         identf = keep.tile([P, P], F32, name="identf")
         nc.vector.tensor_copy(out=identf[:], in_=ident[:])
 
@@ -314,39 +294,44 @@ def tile_memoryefficientpatchdownscale_w_kernel(
             mm1(1, kg)
         for g2 in range(4, 8):
             act(g2)
-        for c in range(2):
+        for c in range(3):
             mm2(0, c)
         for g2 in range(4, 8):
             tr(g2)
             cq(g2)
-        for g2 in range(1, 6):
-            for c in range(2):
+
+        psum_uv = keep.tile([P, 64, 8, 2], F32, name="psum_uv")
+        nc.vector.tensor_tensor(out=psum_uv[:], in0=x_sb[:, :, 0], in1=x_sb[:, :, 1], op=ALU.add)
+        pooled = keep.tile([P, 4, P], F32, name="pooled")
+        nc.vector.tensor_tensor(
+            out=pooled[:].rearrange("p c (s j) -> p (c s) j", j=8),
+            in0=psum_uv[:, :, :, 0],
+            in1=psum_uv[:, :, :, 1],
+            op=ALU.add,
+        )
+        resb = keep.tile([P, 3, 4, P], F32, name="resb")
+        for c in range(3):
+            nc.vector.scalar_tensor_tensor(
+                out=resb[:, c],
+                in0=pooled[:, c, :].unsqueeze(1).to_broadcast([P, 4, P]),
+                scalar=0.25,
+                in1=b2col[:, c, :].unsqueeze(2).to_broadcast([P, 4, P]),
+                op0=ALU.mult,
+                op1=ALU.add,
+            )
+
+        for g2 in range(1, 7):
+            for c in range(3):
                 mm2(g2, c)
-        for c in range(2):
-            for g2 in range(6, 8):
-                mm2(g2, c)
+        for c in range(3):
+            mm2(7, c)
             evac(c)
-        mm2(0, 2)
-        mm2(1, 2)
-        fin(0)
-        mm2(2, 2)
-        mm2(3, 2)
-        fin(1)
-        for g2 in range(4, 8):
-            mm2(g2, 2)
-        evac(2)
-        fin(2)
+        for c in range(3):
+            fin(c)
+        for g2 in range(6):
+            for j in range(4):
+                mm2_tile(g2, j)
         for j in range(4):
-            for g2 in range(4):
-                mm2_tile(g2, j)
-        for j in range(2):
-            for g2 in range(4, 8):
-                mm2_tile(g2, j)
-            fin_tile(j)
-        for g2 in range(4, 6):
-            for j in range(2, 4):
-                mm2_tile(g2, j)
-        for j in range(2, 4):
             for g2 in range(6, 8):
                 mm2_tile(g2, j)
             fin_tile(j)

@@ -34,10 +34,10 @@ def tile_memoryefficientpatchdownscale_w_kernel(
         def bank(k, name):
             return psum.tile([P, N], F32, name=name, tag="b%d" % k)
 
-        s1 = keep.tile([P, HID], U8, name="s1", align_bytes=64)
-        s2 = keep.tile([P, 2, OC], U8, name="s2", align_bytes=64)
-        b1rows = keep.tile([P, N], BF16, name="b1rows")
-        b2rows = keep.tile([P, N], BF16, name="b2rows")
+        s1 = keep.tile([P, HID], U8, name="s1", align_bytes=512)
+        s2 = keep.tile([P, 2, OC], U8, name="s2", align_bytes=512)
+        b1rows = keep.tile([P, N], BF16, name="b1rows", align_bytes=512)
+        b2rows = keep.tile([P, N], BF16, name="b2rows", align_bytes=512)
         warm = keep.tile([P, 1], F32, name="warm")
         warm2 = keep.tile([P, 1], F32, name="warm2")
         ident = keep.tile([P, P], BF16, name="ident")
@@ -55,7 +55,7 @@ def tile_memoryefficientpatchdownscale_w_kernel(
         w1t = {}
         for h in range(2):
             for kg in range(4):
-                w1t[(h, kg)] = keep.tile([P, HID // 2], U32, name="w1_%d_%d" % (h, kg), align_bytes=64)
+                w1t[(h, kg)] = keep.tile([P, HID // 2], U32, name="w1_%d_%d" % (h, kg), align_bytes=512)
 
         for q in range(4):
             nc.gpsimd.dma_start(
@@ -69,10 +69,10 @@ def tile_memoryefficientpatchdownscale_w_kernel(
                     out=s2[32 * q : 32 * q + 16, h, :].bitcast(F32),
                     in_=weight2_scales[4 * h : 4 * h + 4, 4 * q : 4 * q + 4, :].bitcast(F32),
                 )
-        w2_first = keep.tile([P, 1, 3 * N], U32, name="w2_first", align_bytes=64)
+        w2_first = keep.tile([P, 1, 3 * N], U32, name="w2_first", align_bytes=512)
         nc.gpsimd.memset(w2_first[:, 0, 0:16].bitcast(I32), 0)
 
-        x_sb = keep.tile([P, 64, 2, 8, 2], BF16, name="x_sb", align_bytes=64)
+        x_sb = keep.tile([P, 64, 2, 8, 2], BF16, name="x_sb", align_bytes=512)
         x_dst = x_sb[:].rearrange("p (g b i) u j v -> p g b (i u j v)", g=4, b=2)
         for b in range(2):
             nc.sync.dma_start(out=x_dst[:, :, b, :], in_=x[b].rearrange("(g p) h w -> p g (h w)", p=P))
@@ -89,7 +89,7 @@ def tile_memoryefficientpatchdownscale_w_kernel(
             if g0 == 0:
                 t = w2_first
             else:
-                t = keep.tile([P, cnt, N * width], U32, name="w2_%d_%d" % (g0, c0), align_bytes=64)
+                t = keep.tile([P, cnt, N * width], U32, name="w2_%d_%d" % (g0, c0), align_bytes=512)
             src = weight2_words[g0 : g0 + cnt].rearrange("g p n t -> p g (n t)")
             nc.sync.dma_start(
                 out=t[:].bitcast(I32), in_=src[:, :, 4 * N * c0 : 4 * N * (c0 + width)].bitcast(I32)
@@ -99,7 +99,7 @@ def tile_memoryefficientpatchdownscale_w_kernel(
                     w2t[(g0 + gl, c0 + cl)] = t[:, gl, N * cl : N * cl + N]
 
         def load_tiles(g0, cnt, j0, tiles):
-            t = keep.tile([P, cnt, tiles * P], U32, name="w2t_%d_%d" % (g0, j0), align_bytes=64)
+            t = keep.tile([P, cnt, tiles * P], U32, name="w2t_%d_%d" % (g0, j0), align_bytes=512)
             src = weight2_words[g0 : g0 + cnt].rearrange("g p n t -> p g (n t)")
             col0 = 3 * N + P * j0
             nc.sync.dma_start(out=t[:].bitcast(I32), in_=src[:, :, 4 * col0 : 4 * (col0 + tiles * P)].bitcast(I32))
@@ -115,13 +115,13 @@ def tile_memoryefficientpatchdownscale_w_kernel(
         load_tiles(6, 2, 0, 2)
         load_tiles(6, 2, 2, 2)
 
-        grouped = keep.tile([P, 64, 8, 2, 2], BF16, name="grouped", align_bytes=64)
+        grouped = keep.tile([P, 64, 8, 2, 2], BF16, name="grouped", align_bytes=512)
         nc.vector.tensor_copy(
             out=grouped[:].bitcast(F32)[:, :, :, :, 0],
             in_=x_sb[:].bitcast(F32)[:, :, :, :, 0].rearrange("p s u j -> p s j u"),
         )
-        p_codes = keep.tile([P, N], U32, name="p_codes", align_bytes=64)
-        p_plane = keep.tile([P, N], U8, name="p_plane", align_bytes=64)
+        p_codes = keep.tile([P, N], U32, name="p_codes", align_bytes=512)
+        p_plane = keep.tile([P, N], U8, name="p_plane", align_bytes=512)
         nc.vector.quantize_mx(
             out=p_codes[:].bitcast(FP8X4),
             scales=p_plane[:],
@@ -176,11 +176,11 @@ def tile_memoryefficientpatchdownscale_w_kernel(
         identf = keep.tile([P, P], F32, name="identf")
         nc.vector.tensor_copy(out=identf[:], in_=ident[:])
 
-        og = keep.tile([P, 8, P, 4], BF16, name="og", align_bytes=64)
-        o2_codes = keep.tile([P, 8, P], U32, name="o2_codes", align_bytes=64)
-        o2_plane = keep.tile([P, 8, P], U8, name="o2_plane", align_bytes=64)
-        out_sb = keep.tile([P, 3, 2, 4, 64], F32, name="out_sb")
-        out_t = keep.tile([P, 4, P], F32, name="out_t")
+        og = keep.tile([P, 8, P, 4], BF16, name="og", align_bytes=512)
+        o2_codes = keep.tile([P, 8, P], U32, name="o2_codes", align_bytes=512)
+        o2_plane = keep.tile([P, 8, P], U8, name="o2_plane", align_bytes=512)
+        out_sb = keep.tile([P, 3, 2, 4, 64], F32, name="out_sb", align_bytes=512)
+        out_t = keep.tile([P, 4, P], F32, name="out_t", align_bytes=512)
         banks = {}
         o2s = {}
         pts = {}

from contextlib import ExitStack

import concourse.mybir as mybir
from concourse.masks import make_identity

F32 = mybir.dt.float32
BF16 = mybir.dt.bfloat16
I32 = mybir.dt.int32
U32 = mybir.dt.uint32
U8 = mybir.dt.uint8
FP8X4 = mybir.dt.float8_e4m3fn_x4
ACT = mybir.ActivationFunctionType
ALU = mybir.AluOpType

P = 128
HID = 4096
OC = 2048
K1 = 2048
FLOPS = 2 * P * K1 * HID + 2 * P * HID * OC

N = 512


def tile_memoryefficientpatchdownscale_w_kernel(
    tc, x, weight1_words, weight1_scales, bias1, weight2_words, weight2_scales, bias2, out
):
    nc = tc.nc
    with ExitStack() as ctx:
        keep = ctx.enter_context(tc.tile_pool(name="keep", bufs=1))
        work = ctx.enter_context(tc.tile_pool(name="work", bufs=4))
        psum = ctx.enter_context(tc.psum_pool(name="psum", bufs=1))
        ctx.enter_context(tc.manual_schedule())

        def bank(k, name):
            return psum.tile([P, N], F32, name=name, tag="b%d" % k)

        s1 = keep.tile([P, HID], U8, name="s1", align_bytes=512)
        s2 = keep.tile([P, 2, OC], U8, name="s2", align_bytes=512)
        b1rows = keep.tile([P, N], BF16, name="b1rows", align_bytes=512)
        b2rows = keep.tile([P, N], BF16, name="b2rows", align_bytes=512)
        warm = keep.tile([P, 1], F32, name="warm")
        warm2 = keep.tile([P, 1], F32, name="warm2")
        ident = keep.tile([P, P], BF16, name="ident")
        make_identity(nc, ident[:])
        nc.vector.memset(s1[:].bitcast(I32), 0)
        nc.vector.memset(b1rows[:], 0.0)
        nc.vector.memset(b2rows[:], 0.0)
        nc.vector.memset(warm[:], 0.0)
        rsel = keep.tile([P, P, 4], BF16, name="rsel")
        nc.vector.tensor_scalar_mul(out=rsel[:], in0=ident[:].unsqueeze(2).to_broadcast([P, P, 4]), scalar1=0.25)
        rflat = rsel[:].rearrange("c q r -> c (q r)")
        nc.vector.memset(s2[:].bitcast(I32), 0)
        nc.scalar.activation(out=warm2[:], in_=warm[:], func=ACT.Silu)

        w1t = {}
        for h in range(2):
            for kg in range(4):
                w1t[(h, kg)] = keep.tile([P, HID // 2], U32, name="w1_%d_%d" % (h, kg), align_bytes=512)

        for q in range(4):
            nc.gpsimd.dma_start(
                out=s1[32 * q : 32 * q + 16, :].bitcast(F32),
                in_=weight1_scales[:, 4 * q : 4 * q + 4, :].bitcast(F32),
            )
        nc.gpsimd.memset(w1t[(0, 3)][:, 0:16].bitcast(I32), 0)
        for h in range(2):
            for q in range(4):
                nc.gpsimd.dma_start(
                    out=s2[32 * q : 32 * q + 16, h, :].bitcast(F32),
                    in_=weight2_scales[4 * h : 4 * h + 4, 4 * q : 4 * q + 4, :].bitcast(F32),
                )
        w2_first = keep.tile([P, 1, 3 * N], U32, name="w2_first", align_bytes=512)
        nc.gpsimd.memset(w2_first[:, 0, 0:16].bitcast(I32), 0)

        x_sb = keep.tile([P, 64, 2, 8, 2], BF16, name="x_sb", align_bytes=512)
        x_dst = x_sb[:].rearrange("p (g b i) u j v -> p g b (i u j v)", g=4, b=2)
        for b in range(2):
            nc.sync.dma_start(out=x_dst[:, :, b, :], in_=x[b].rearrange("(g p) h w -> p g (h w)", p=P))
        for h in range(2):
            for kg in range(4):
                src = weight1_words[kg].rearrange("p n t -> p (n t)")[:, 2 * HID * h : 2 * HID * (h + 1)]
                nc.sync.dma_start(out=w1t[(h, kg)][:].bitcast(I32), in_=src.bitcast(I32))
                if h == 0 and kg == 0:
                    nc.sync.dma_start(out=b1rows[0:8, :], in_=bias1.rearrange("(g f) -> g f", f=N))
                    nc.sync.dma_start(out=b2rows[0:4, :], in_=bias2.rearrange("(g f) -> g f", f=N))
        w2t = {}

        def load_w2(g0, cnt, c0, width):
            if g0 == 0:
                t = w2_first
            else:
                t = keep.tile([P, cnt, N * width], U32, name="w2_%d_%d" % (g0, c0), align_bytes=512)
            src = weight2_words[g0 : g0 + cnt].rearrange("g p n t -> p g (n t)")
            nc.sync.dma_start(
                out=t[:].bitcast(I32), in_=src[:, :, 4 * N * c0 : 4 * N * (c0 + width)].bitcast(I32)
            )
            for gl in range(cnt):
                for cl in range(width):
                    w2t[(g0 + gl, c0 + cl)] = t[:, gl, N * cl : N * cl + N]

        def load_tiles(g0, cnt, j0, tiles):
            t = keep.tile([P, cnt, tiles * P], U32, name="w2t_%d_%d" % (g0, j0), align_bytes=512)
            src = weight2_words[g0 : g0 + cnt].rearrange("g p n t -> p g (n t)")
            col0 = 3 * N + P * j0
            nc.sync.dma_start(out=t[:].bitcast(I32), in_=src[:, :, 4 * col0 : 4 * (col0 + tiles * P)].bitcast(I32))
            for gl in range(cnt):
                for jl in range(tiles):
                    w2j[(g0 + gl, j0 + jl)] = t[:, gl, P * jl : P * jl + P]

        w2j = {}
        for g2 in range(8):
            load_w2(g2, 1, 0, 3)
        load_tiles(0, 4, 0, 4)
        load_tiles(4, 2, 0, 4)
        load_tiles(6, 2, 0, 2)
        load_tiles(6, 2, 2, 2)

        grouped = keep.tile([P, 64, 8, 2, 2], BF16, name="grouped", align_bytes=512)
        nc.vector.tensor_copy(
            out=grouped[:].bitcast(F32)[:, :, :, :, 0],
            in_=x_sb[:].bitcast(F32)[:, :, :, :, 0].rearrange("p s u j -> p s j u"),
        )
        p_codes = keep.tile([P, N], U32, name="p_codes", align_bytes=512)
        p_plane = keep.tile([P, N], U8, name="p_plane", align_bytes=512)
        nc.vector.quantize_mx(
            out=p_codes[:].bitcast(FP8X4),
            scales=p_plane[:],
            in_=grouped[:].rearrange("p s j u v -> p (s j u v)"),
        )

        b1bc = keep.tile([P, 8, 4, P], BF16, name="b1bc")
        for g in range(8):
            ps = bank(4 + g % 4, "ps_b1")
            nc.tensor.matmul(
                out=ps[:], lhsT=ident[:, g : g + 1].to_broadcast([P, P]), rhs=b1rows[:], start=True, stop=True
            )
            nc.scalar.copy(out=b1bc[:, g], in_=ps[:].rearrange("m (p t) -> m t p", t=4))

        ps_b2 = bank(0, "ps_b2")
        for e in range(4):
            nc.tensor.transpose(
                ps_b2[:].bitcast(BF16)[:, P * e : P * e + P],
                b2rows[:].rearrange("r (n e) -> r e n", e=4)[:, e, :],
                ident[:],
            )
        b2col = keep.tile([P, 4, 4], F32, name="b2col")
        nc.vector.tensor_copy(
            out=b2col[:],
            in_=ps_b2[:].bitcast(BF16)[:, 0 : 4 * P].rearrange("p (e r) -> p r e", e=4)[:, 0:4, :],
        )

        ps_b2t = bank(1, "ps_b2")
        for j in range(4):
            nc.tensor.transpose(ps_b2t[:].bitcast(BF16)[:, P * j : P * j + P], b2rows[:, P * j : P * j + P], ident[:])
        b2t = keep.tile([P, 4], F32, name="b2t")
        nc.vector.tensor_copy(
            out=b2t[:], in_=ps_b2t[:].bitcast(BF16)[:, 0 : 4 * P].rearrange("p (j r) -> p r j", j=4)[:, 3, :]
        )
        resb_t = keep.tile([P, 4, P], F32, name="resb_t")
        ps_res = bank(2, "ps_res")
        for j in range(4):
            for n in range(4):
                nc.tensor.matmul(
                    out=ps_res[:, P * j : P * j + P].rearrange("o (s j) -> o s j", j=8),
                    lhsT=rflat[:, P * j : P * j + P],
                    rhs=x_sb[:, 48:64, n // 2, :, n % 2],
                    start=(n == 0),
                    stop=(n == 3),
                )
        nc.vector.tensor_tensor(
            out=resb_t[:],
            in0=ps_res[:].rearrange("o (j t) -> o j t", j=4),
            in1=b2t[:].unsqueeze(2).to_broadcast([P, 4, P]),
            op=ALU.add,
        )
        identf = keep.tile([P, P], F32, name="identf")
        nc.vector.tensor_copy(out=identf[:], in_=ident[:])

        og = keep.tile([P, 8, P, 4], BF16, name="og", align_bytes=512)
        o2_codes = keep.tile([P, 8, P], U32, name="o2_codes", align_bytes=512)
        o2_plane = keep.tile([P, 8, P], U8, name="o2_plane", align_bytes=512)
        out_sb = keep.tile([P, 3, 2, 4, 64], F32, name="out_sb", align_bytes=512)
        out_t = keep.tile([P, 4, P], F32, name="out_t", align_bytes=512)
        banks = {}
        o2s = {}
        pts = {}
        accs = {}
        o3s = {}

        def mm1(h, kg):
            for n in range(4):
                g2 = 4 * h + n
                if kg == 0:
                    banks[g2] = bank(g2, "ps_o1")
                nc.tensor.matmul_mx(
                    out=banks[g2][:],
                    lhsT=p_codes[:, P * kg : P * kg + P].bitcast(FP8X4),
                    lhsT_scale=p_plane[:, P * kg : P * kg + P],
                    rhs=w1t[(h, kg)][:, N * n : N * n + N].bitcast(FP8X4),
                    rhs_scale=s1[4 * kg : P, N * g2 : N * g2 + N],
                    start=(kg == 0),
                    stop=(kg == 3),
                )

        def act(g2):
            o1 = work.tile([P, 4, P], F32, name="o1")
            nc.vector.tensor_tensor(
                out=o1[:], in0=banks[g2][:].rearrange("m (p t) -> m t p", t=4), in1=b1bc[:, g2], op=ALU.add
            )
            o2 = work.tile([P, 4, P], BF16, name="o2")
            nc.scalar.activation(out=o2[:], in_=o1[:], func=ACT.Silu)
            o2s[g2] = o2

        def tr(g2):
            pt = bank(g2 % 4 if g2 < 4 else g2 % 3, "ps_t")
            for t in range(4):
                nc.tensor.transpose(pt[:].bitcast(BF16)[:, P * t : P * t + P], o2s[g2][:, t, :], ident[:])
            pts[g2] = pt

        def cq(g2):
            nc.scalar.copy(
                out=og[:, g2], in_=pts[g2][:].bitcast(BF16)[:, 0:N].rearrange("p (t r) -> p r t", t=4)
            )
            nc.vector.quantize_mx(
                out=o2_codes[:, g2, :].bitcast(FP8X4),
                scales=o2_plane[:, g2, :],
                in_=og[:, g2].rearrange("p r t -> p (r t)"),
            )

        def mm2(g2, c):
            if g2 == 0:
                accs[c] = bank(4 + c, "ps_o3")
            nc.tensor.matmul_mx(
                out=accs[c][:],
                lhsT=o2_codes[:, g2, :].bitcast(FP8X4),
                lhsT_scale=o2_plane[:, g2, :],
                rhs=w2t[(g2, c)].bitcast(FP8X4),
                rhs_scale=s2[4 * (g2 % 4) : P, g2 // 4, N * c : N * c + N],
                start=(g2 == 0),
                stop=(g2 == 7),
            )

        def evac(c):
            o3s[c] = work.tile([P, 4, P], F32, name="o3")
            nc.scalar.copy(out=o3s[c][:], in_=accs[c][:].rearrange("m (n e) -> m e n", e=4))

        def fin(c):
            o3 = o3s[c]
            pt = bank(c, "ps_f")
            for e in range(4):
                nc.tensor.transpose(pt[:, P * e : P * e + P], o3[:, e, :], identf[:])
            nc.vector.tensor_tensor(
                out=out_sb[:, c].rearrange("p b e s -> p e b s"),
                in0=pt[:].rearrange("p (e b s) -> p e b s", e=4, b=2),
                in1=resb[:, c].rearrange("p e (b s) -> p e b s", b=2),
                op=ALU.add,
            )
            nc.sync.dma_start(
                out=out[:, N * c : N * c + N].rearrange("b (p e) h w -> p b (e h w)", e=4),
                in_=out_sb[:, c].rearrange("p b e s -> p b (e s)"),
            )

        def mm2_tile(g2, j):
            if g2 == 0:
                accs[4 + j] = bank((7, 5, 3, 4)[j], "ps_o3")
            col0 = 3 * N + P * j
            nc.tensor.matmul_mx(
                out=accs[4 + j][:, 0:P],
                lhsT=w2j[(g2, j)].bitcast(FP8X4),
                lhsT_scale=s2[4 * (g2 % 4) : P, g2 // 4, col0 : col0 + P],
                rhs=o2_codes[:, g2, :].bitcast(FP8X4),
                rhs_scale=o2_plane[:, g2, :],
                start=(g2 == 0),
                stop=(g2 == 7),
            )

        def fin_tile(j):
            nc.vector.tensor_tensor(out=out_t[:, j, :], in0=accs[4 + j][:, 0:P], in1=resb_t[:, j, :], op=ALU.add)
            col0 = 3 * N + P * j
            nc.sync.dma_start(
                out=out[:, col0 : col0 + P].rearrange("b o h w -> o b (h w)"),
                in_=out_t[:, j, :].rearrange("o (b s) -> o b s", b=2),
            )

        for kg in range(4):
            mm1(0, kg)
        for g2 in range(4):
            act(g2)
        mm1(1, 0)
        for g2 in range(4):
            tr(g2)
            cq(g2)
        for kg in range(1, 4):
            mm1(1, kg)
        for g2 in range(4, 8):
            act(g2)
        for c in range(3):
            mm2(0, c)
        for g2 in range(4, 8):
            tr(g2)
            cq(g2)

        psum_uv = keep.tile([P, 64, 8, 2], F32, name="psum_uv")
        nc.vector.tensor_tensor(out=psum_uv[:], in0=x_sb[:, :, 0], in1=x_sb[:, :, 1], op=ALU.add)
        pooled = keep.tile([P, 4, P], F32, name="pooled")
        nc.vector.tensor_tensor(
            out=pooled[:].rearrange("p c (s j) -> p (c s) j", j=8),
            in0=psum_uv[:, :, :, 0],
            in1=psum_uv[:, :, :, 1],
            op=ALU.add,
        )
        resb = keep.tile([P, 3, 4, P], F32, name="resb")
        for c in range(3):
            nc.vector.scalar_tensor_tensor(
                out=resb[:, c],
                in0=pooled[:, c, :].unsqueeze(1).to_broadcast([P, 4, P]),
                scalar=0.25,
                in1=b2col[:, c, :].unsqueeze(2).to_broadcast([P, 4, P]),
                op0=ALU.mult,
                op1=ALU.add,
            )

        for g2 in range(1, 7):
            for c in range(3):
                mm2(g2, c)
        for c in range(3):
            mm2(7, c)
            evac(c)
        for c in range(3):
            fin(c)
        for g2 in range(6):
            for j in range(4):
                mm2_tile(g2, j)
        for j in range(4):
            for g2 in range(6, 8):
                mm2_tile(g2, j)
            fin_tile(j)
